import numpy as np
import ml_dtypes


def mxq(x, axis, fmt="e4m3"):
    dtype, down = {"e4m3": (ml_dtypes.float8_e4m3fn, 7), "e5m2": (ml_dtypes.float8_e5m2, 14)}[fmt]
    v = np.moveaxis(np.asarray(x, np.float32).astype(ml_dtypes.bfloat16).astype(np.float64), axis, -1)
    blocks = v.reshape(v.shape[:-1] + (-1, 32))
    amax = np.abs(blocks).max(-1, keepdims=True)
    byte = np.maximum(np.where(amax > 0, np.frexp(amax)[1] - 1 + 127, 0) - down, 1)
    scale = np.exp2(byte - 127.0)
    codes = (blocks / scale).astype(np.float32).astype(dtype).astype(np.float64)
    return np.moveaxis((codes * scale).reshape(v.shape), -1, axis)


WIDE = False


def mx_kscale(k):
    if not WIDE:
        return np.ones(k)
    levels = np.array([10, -10, 5, -5, 0])
    a = np.random.permutation(np.resize(levels, k // 512 * 4)).reshape(k // 512, 4)
    idx = np.arange(k)
    return np.exp2(a[idx // 512, idx % 128 // 32])


BF16 = ml_dtypes.bfloat16


def bf(x):
    return np.asarray(x, np.float32).astype(BF16)


def f64(x):
    return np.asarray(x).astype(np.float64)


B, D, T, DEPTH, LD = 512, 1024, 128, 6, 128
NI = 2 ** DEPTH - 1
NL = 2 ** DEPTH


def sigmoid(v):
    return 1.0 / (1.0 + np.exp(-v))


def setup_inputs():
    s = mx_kscale(D)
    return {"x": bf(np.random.standard_normal((B, D)) * s),
            "W": bf(np.random.standard_normal((NI, T, D)) / np.sqrt(D) / s),
            "b": bf(np.random.standard_normal((NI, T)) * 0.5),
            "leaf_w": bf(np.random.standard_normal((NL, LD, T)) / np.sqrt(T * 0.6 ** DEPTH))}


def reference(x, W, b, leaf_w):
    wq = mxq(f64(W).reshape(NI * T, D), 1, "e4m3")
    z = (mxq(f64(x), 1, "e4m3") @ wq.T).reshape(B, NI, T) + f64(b)
    gates = sigmoid(z)
    probs = np.ones((B, 1, T))
    for l in range(DEPTH):
        g = gates[:, 2 ** l - 1: 2 ** (l + 1) - 1]
        probs = np.stack([probs * g, probs * (1.0 - g)], axis=2).reshape(B, 2 ** (l + 1), T)
    lw = f64(leaf_w).transpose(0, 2, 1).reshape(NL * T, LD)
    return mxq(probs.reshape(B, NL * T), 1, "e4m3") @ mxq(lw, 0, "e4m3")

@@ -1,0 +1,345 @@
+from contextlib import ExitStack
+
+import concourse.mybir as mybir
+from concourse.masks import make_identity
+
+F32 = mybir.dt.float32
+BF16 = mybir.dt.bfloat16
+U32 = mybir.dt.uint32
+U8 = mybir.dt.uint8
+FP8X4 = mybir.dt.float8_e4m3fn_x4
+ALU = mybir.AluOpType
+ACT = mybir.ActivationFunctionType
+
+P = 128
+B, D, T, LD = 512, 1024, 128, 128
+NI, NL = 63, 64
+FLOPS = 2 * B * D * NI * T + 2 * B * NL * T * LD
+
+PINNED = False
+H_ON_VECTOR = 1
+
+
+def build_units():
+    units = [
+        dict(n0=0, nn=3, kind="top", par="p1", pj=0, ch="p2", cj=0),
+        dict(n0=3, nn=4, kind="mid", par="p2", pj=0, ch="p3", cj=0),
+        dict(n0=7, nn=4, kind="mid", par="p3", pj=0, ch="p4", cj=0),
+        dict(n0=11, nn=4, kind="mid", par="p3", pj=4, ch="p4", cj=4),
+    ]
+    for a in range(4):
+        units.append(dict(n0=15 + 4 * a, nn=4, kind="mid", par="p4", pj=4 * a, ch="p5", cj=0))
+        for hf in range(2):
+            units.append(dict(n0=31 + 8 * a + 4 * hf, nn=4, kind="leaf", par="p5", pj=4 * hf, q0=2 * (2 * a + hf)))
+    return units
+
+
+def tile_softtreeensemble_pa_kernel(tc, x, W, b, leaf_w, out):
+    nc = tc.nc
+    units = build_units()
+    nu = len(units)
+    with ExitStack() as ctx:
+        const = ctx.enter_context(tc.tile_pool(name="const", bufs=1))
+        rawp = ctx.enter_context(tc.tile_pool(name="rawp", bufs=4))
+        grpp = ctx.enter_context(tc.tile_pool(name="grpp", bufs=3))
+        lgp = ctx.enter_context(tc.tile_pool(name="lgp", bufs=2))
+        wcp = ctx.enter_context(tc.tile_pool(name="wcp", bufs=2))
+        gp = ctx.enter_context(tc.tile_pool(name="gp", bufs=3))
+        hp = ctx.enter_context(tc.tile_pool(name="hp", bufs=2))
+        pp = ctx.enter_context(tc.tile_pool(name="pp", bufs=2))
+        p4p = ctx.enter_context(tc.tile_pool(name="p4p", bufs=1))
+        p6p = ctx.enter_context(tc.tile_pool(name="p6p", bufs=2))
+        ps_t = ctx.enter_context(tc.psum_pool(name="ps_t", bufs=4))
+        ps_z = ctx.enter_context(tc.psum_pool(name="ps_z", bufs=3))
+        ps_o = ctx.enter_context(tc.psum_pool(name="ps_o", bufs=1))
+        if PINNED:
+            ctx.enter_context(tc.manual_schedule())
+
+        ident32 = const.tile([P, P], F32, name="ident32")
+        make_identity(nc, ident32[:])
+        ident16 = const.tile([P, P], BF16, name="ident16")
+        make_identity(nc, ident16[:])
+        brows = const.tile([P, P], BF16, name="brows")
+        nc.vector.memset(brows[:], 0.0)
+        bias = const.tile([P, P], F32, name="bias")
+        nbias = const.tile([P, P], F32, name="nbias")
+        xc = const.tile([P, 1024], U32, name="xc", align_bytes=64)
+        xs = const.tile([P, 1024], U8, name="xs", align_bytes=64)
+        lwc = const.tile([P, 2048], U32, name="lwc", align_bytes=64)
+        lws = const.tile([P, 2048], U8, name="lws", align_bytes=64)
+
+        raw = {}
+        wg = {}
+        wcs = {}
+        gts = {}
+        hts = {}
+        pt = {}
+        p6 = {}
+        lraw = {}
+        lgs = {}
+
+        def load_w(u):
+            if u >= nu:
+                return
+            n0, nn = units[u]["n0"], units[u]["nn"]
+            r = rawp.tile([P, 4096], BF16, name="raw%d" % u, tag="raw")
+            nc.sync.dma_start(
+                out=r[:, : nn * 1024].rearrange("p (n d) -> p n d", n=nn),
+                in_=W[n0 : n0 + nn].rearrange("n t d -> t n d"),
+            )
+            raw[u] = r
+
+        def load_leaf(hh):
+            r = rawp.tile([P, 4096], BF16, name="lraw%d" % hh, tag="raw")
+            nc.sync.dma_start(
+                out=r[:].rearrange("p (j t) -> p j t", j=32),
+                in_=leaf_w[32 * hh : 32 * hh + 32].rearrange("j c t -> c j t"),
+            )
+            lraw[hh] = r
+
+        def halves(u):
+            nn = units[u]["nn"]
+            if nn == 3:
+                return [[0], [1, 2]]
+            return [[0, 1], [2, 3]]
+
+        def transpose_copy_w(u, half):
+            if u >= nu:
+                return
+            if half == 0:
+                wg[u] = grpp.tile([P, 2048], F32, name="wg%d" % u, tag="grp", align_bytes=64)
+            rw = raw[u][:].bitcast(F32)
+            banks = []
+            for e in halves(u)[half]:
+                wt = ps_t.tile([P, 512], F32, name="wt%d_%d" % (u, e), tag="wt")
+                for s in range(4):
+                    nc.tensor.transpose(wt[:, 128 * s : 128 * s + 128], rw[:, 512 * e + 128 * s : 512 * e + 128 * s + 128], ident32[:])
+                banks.append((e, wt))
+            for e, wt in banks:
+                nc.scalar.copy(
+                    out=wg[u][:, 512 * e : 512 * e + 512].rearrange("p (g m u) -> p g m u", g=2, u=2),
+                    in_=wt[:].rearrange("p (g u m) -> p g m u", g=2, u=2),
+                )
+
+        def quant_w(u):
+            if u >= nu:
+                return
+            nn = units[u]["nn"]
+            c = wcp.tile([P, 1024], U32, name="wc%d" % u, tag="wc", align_bytes=64)
+            s = wcp.tile([P, 1024], U8, name="ws%d" % u, tag="ws", align_bytes=64)
+            wcs[u] = (c, s)
+            parts = [(0, 4)] if nn == 4 else [(0, 1), (1, 2)]
+            for e0, ne in parts:
+                nc.vector.quantize_mx(
+                    out=c[:, 256 * e0 : 256 * (e0 + ne)].bitcast(FP8X4),
+                    scales=s[:, 256 * e0 : 256 * (e0 + ne)],
+                    in_=wg[u][:, 512 * e0 : 512 * (e0 + ne)].bitcast(BF16),
+                )
+
+        def gates(u, half):
+            if u >= nu:
+                return
+            un = units[u]
+            if half == 0:
+                gts[u] = gp.tile([P, 2048], F32, name="g%d" % u, tag="g")
+                if un["kind"] == "leaf":
+                    hts[u] = hp.tile([P, 2048], F32, name="h%d" % u, tag="h")
+                if un["kind"] == "top":
+                    pt["p1"] = pp.tile([P, 4096], F32, name="p1", tag="p8")
+            c, s = wcs[u]
+            zs = []
+            for e in halves(u)[half]:
+                z = ps_z.tile([P, 512], F32, name="z%d_%d" % (u, e), tag="z")
+                for g in range(2):
+                    cols = slice(256 * e + 128 * g, 256 * e + 128 * g + 128)
+                    nc.tensor.matmul_mx(
+                        out=z[:],
+                        lhsT=c[:, cols].bitcast(FP8X4),
+                        lhsT_scale=s[:, cols],
+                        rhs=xc[:, 512 * g : 512 * g + 512].bitcast(FP8X4),
+                        rhs_scale=xs[:, 512 * g : 512 * g + 512],
+                        start=(g == 0),
+                        stop=(g == 1),
+                    )
+                zs.append((e, z))
+            for e, z in zs:
+                n = un["n0"] + e
+                if n == 0:
+                    nc.scalar.activation(out=pt["p1"][:, 0:512], in_=z[:], func=ACT.Sigmoid, bias=bias[:, 0:1], scale=1.0)
+                    nc.scalar.activation(out=pt["p1"][:, 512:1024], in_=z[:], func=ACT.Sigmoid, bias=nbias[:, 0:1], scale=-1.0)
+                    continue
+                nc.scalar.activation(out=gts[u][:, 512 * e : 512 * e + 512], in_=z[:], func=ACT.Sigmoid, bias=bias[:, n : n + 1], scale=1.0)
+                if un["kind"] == "leaf" and e < 4 - H_ON_VECTOR:
+                    nc.scalar.activation(out=hts[u][:, 512 * e : 512 * e + 512], in_=z[:], func=ACT.Sigmoid, bias=nbias[:, n : n + 1], scale=-1.0)
+
+        def tree_a(u):
+            if u < 0 or u >= nu:
+                return
+            un = units[u]
+            if un["kind"] == "leaf":
+                par = pt["p5"][:, 512 * un["pj"] : 512 * un["pj"] + 2048].rearrange("p (t c i) -> p c t i", t=4, i=4)
+                if H_ON_VECTOR:
+                    lo = 512 * (4 - H_ON_VECTOR)
+                    nc.vector.tensor_scalar(out=hts[u][:, lo:2048], in0=gts[u][:, lo:2048], scalar1=-1.0, scalar2=1.0, op0=ALU.mult, op1=ALU.add)
+                pg = p6p.tile([P, 4096], BF16, name="p6g%d" % u, tag="p6g", align_bytes=64)
+                p6[u] = pg
+                nc.vector.tensor_tensor(
+                    out=pg[:, 0:2048].rearrange("p (c i t) -> p c t i", i=4, t=4),
+                    in0=par,
+                    in1=gts[u][:].rearrange("p (t c i) -> p c t i", t=4, i=4),
+                    op=ALU.mult,
+                )
+                nc.vector.tensor_tensor(
+                    out=pg[:, 2048:4096].rearrange("p (c i t) -> p c t i", i=4, t=4),
+                    in0=par,
+                    in1=hts[u][:].rearrange("p (t c i) -> p c t i", t=4, i=4),
+                    op=ALU.mult,
+                )
+                return
+            nn = 2 if un["kind"] == "top" else 4
+            g0 = 512 if un["kind"] == "top" else 0
+            if un["cj"] == 0:
+                if un["ch"] == "p4":
+                    pt["p4"] = p4p.tile([P, 8192], F32, name="p4")
+                else:
+                    pt[un["ch"]] = pp.tile([P, 4096], F32, name="%s_%d" % (un["ch"], u), tag="p8")
+            par = pt[un["par"]][:, 512 * un["pj"] : 512 * (un["pj"] + nn)].rearrange("p (j w) -> p j w", w=512)
+            chv = pt[un["ch"]][:, 1024 * un["cj"] : 1024 * (un["cj"] + nn)].rearrange("p (j b w) -> p j b w", b=2, w=512)
+            nc.vector.tensor_tensor(
+                out=chv[:, :, 0, :],
+                in0=par,
+                in1=gts[u][:, g0 : g0 + 512 * nn].rearrange("p (j w) -> p j w", w=512),
+                op=ALU.mult,
+            )
+
+        def tree_b(u):
+            if u < 0 or u >= nu:
+                return
+            un = units[u]
+            if un["kind"] == "leaf":
+                c = p6p.tile([P, 1024], U32, name="p6c%d" % u, tag="p6c", align_bytes=64)
+                s = p6p.tile([P, 1024], U8, name="p6s%d" % u, tag="p6s", align_bytes=64)
+                for bb in range(2):
+                    nc.vector.quantize_mx(
+                        out=c[:, 512 * bb : 512 * bb + 512].bitcast(FP8X4),
+                        scales=s[:, 512 * bb : 512 * bb + 512],
+                        in_=p6[u][:, 2048 * bb : 2048 * bb + 2048],
+                    )
+                p6[u] = (c, s)
+                return
+            nn = 2 if un["kind"] == "top" else 4
+            par = pt[un["par"]][:, 512 * un["pj"] : 512 * (un["pj"] + nn)].rearrange("p (j w) -> p j w", w=512)
+            chv = pt[un["ch"]][:, 1024 * un["cj"] : 1024 * (un["cj"] + nn)].rearrange("p (j b w) -> p j b w", b=2, w=512)
+            nc.vector.tensor_tensor(out=chv[:, :, 1, :], in0=par, in1=chv[:, :, 0, :], op=ALU.subtract)
+
+        o_ps = ps_o.tile([P, 512], F32, name="o_ps")
+
+        def second(u):
+            if u < 0 or u >= nu or units[u]["kind"] != "leaf":
+                return
+            c, s = p6[u]
+            for bb in range(2):
+                q = units[u]["q0"] + bb
+                nc.tensor.matmul_mx(
+                    out=o_ps[:],
+                    lhsT=lwc[:, 128 * q : 128 * q + 128].bitcast(FP8X4),
+                    lhsT_scale=lws[:, 128 * q : 128 * q + 128],
+                    rhs=c[:, 512 * bb : 512 * bb + 512].bitcast(FP8X4),
+                    rhs_scale=s[:, 512 * bb : 512 * bb + 512],
+                    start=(q == 0),
+                    stop=(q == 15),
+                )
+
+        def leaf_tc(piece):
+            hh = piece // 2
+            lg = lgp.tile([P, 2048], BF16, name="lg%d" % piece, tag="lg", align_bytes=64)
+            lgs[piece] = lg
+            banks = []
+            for k in range(2):
+                a = 2 * piece + k
+                bank = ps_t.tile([P, 1024], BF16, name="lt%d" % a, tag="wt")
+                for bb in range(2):
+                    for t in range(4):
+                        jl = 8 * a + 2 * t + bb - 32 * hh
+                        nc.tensor.transpose(bank[:, (4 * bb + t) * 128 : (4 * bb + t) * 128 + 128], lraw[hh][:, 128 * jl : 128 * jl + 128], ident16[:])
+                banks.append(bank)
+            for k in range(2):
+                nc.scalar.copy(
+                    out=lg[:, 1024 * k : 1024 * k + 1024].rearrange("p (b c t) -> p b c t", b=2, t=4),
+                    in_=banks[k][:].rearrange("p (b t c) -> p b c t", b=2, t=4),
+                )
+
+        def leaf_q(piece):
+            nc.vector.quantize_mx(
+                out=lwc[:, 512 * piece : 512 * piece + 512].bitcast(FP8X4),
+                scales=lws[:, 512 * piece : 512 * piece + 512],
+                in_=lgs[piece][:],
+            )
+
+        xraw = rawp.tile([P, 4096], BF16, name="xraw", tag="raw")
+        xv = x.rearrange("(k p) d -> p k d", p=P)
+        for kk in range(2):
+            nc.sync.dma_start(
+                out=xraw[:, 2048 * kk : 2048 * kk + 2048].rearrange("p (k d) -> p k d", k=2),
+                in_=xv[:, 2 * kk : 2 * kk + 2, :],
+            )
+        nc.scalar.dma_start(out=brows[0:NI, :], in_=b)
+        load_w(0)
+        load_w(1)
+        load_w(2)
+
+        xw = xraw[:].bitcast(F32)
+        xg = grpp.tile([P, 2048], F32, name="xg", tag="grp", align_bytes=64)
+        for kk in range(2):
+            for g in range(2):
+                bank = ps_t.tile([P, 512], F32, name="xt%d_%d" % (kk, g), tag="wt")
+                for k2 in range(2):
+                    for u2 in range(2):
+                        src = 512 * (2 * kk + k2) + 256 * g + 128 * u2
+                        nc.tensor.transpose(bank[:, (2 * k2 + u2) * 128 : (2 * k2 + u2) * 128 + 128], xw[:, src : src + 128], ident32[:])
+                dst = xg[:, 1024 * g + 512 * kk : 1024 * g + 512 * kk + 512].rearrange("p (k i u) -> p k i u", k=2, u=2)
+                srcv = bank[:].rearrange("p (k u i) -> p k i u", k=2, u=2)
+                if g == 0:
+                    nc.vector.tensor_copy(out=dst, in_=srcv)
+                else:
+                    nc.scalar.copy(out=dst, in_=srcv)
+        bt = ps_t.tile([P, 1024], BF16, name="bt", tag="wt")
+        nc.tensor.transpose(bt[:, 0:128], brows[:], ident16[:])
+        nc.vector.tensor_copy(out=bias[:], in_=bt[:, 0:128])
+        nc.vector.tensor_scalar(out=nbias[:], in0=bias[:], scalar1=-1.0, scalar2=0.0, op0=ALU.mult, op1=ALU.add)
+        nc.vector.quantize_mx(out=xc[:].bitcast(FP8X4), scales=xs[:], in_=xg[:].bitcast(BF16))
+
+        for u in range(2):
+            for half in range(2):
+                transpose_copy_w(u, half)
+        quant_w(0)
+
+        for it in range(nu + 2):
+            if it == 0:
+                load_leaf(0)
+            if it == 2:
+                load_leaf(1)
+            load_w(it + 3)
+            for half in range(2):
+                gates(it, half)
+                if half == 0:
+                    second(it - 2)
+                transpose_copy_w(it + 2, half)
+            if 1 <= it <= 4:
+                leaf_tc(it - 1)
+            tree_a(it - 1)
+            quant_w(it + 1)
+            if 2 <= it <= 5:
+                leaf_q(it - 2)
+            tree_b(it - 1)
+
+        o_t = hp.tile([P, 2048], F32, name="o_t", tag="h")
+        nc.vector.tensor_copy(out=o_t[:, 0:512], in_=o_ps[:])
+        o_b = ps_t.tile([P, 512], F32, name="o_b", tag="wt")
+        for k in range(4):
+            nc.tensor.transpose(o_b[:, 128 * k : 128 * k + 128], o_t[:, 128 * k : 128 * k + 128], ident32[:])
+        nc.vector.tensor_copy(out=o_t[:, 512:1024], in_=o_b[:])
+        nc.sync.dma_start(
+            out=out.rearrange("(k p) c -> p k c", p=P),
+            in_=o_t[:, 512:1024].rearrange("p (k c) -> p k c", k=4),
+        )

@@ -17,7 +17,8 @@ NI, NL = 63, 64
 FLOPS = 2 * B * D * NI * T + 2 * B * NL * T * LD
 
 PINNED = False
-H_ON_VECTOR = 1
+LEAF_LOAD_AT = [3, 5, 8, 11]
+LEAF_WORK_AT = [4, 7, 10, 13]
 
 
 def build_units():
@@ -45,7 +46,6 @@ def tile_softtreeensemble_pa_kernel(tc, x, W, b, leaf_w, out):
         lgp = ctx.enter_context(tc.tile_pool(name="lgp", bufs=2))
         wcp = ctx.enter_context(tc.tile_pool(name="wcp", bufs=2))
         gp = ctx.enter_context(tc.tile_pool(name="gp", bufs=3))
-        hp = ctx.enter_context(tc.tile_pool(name="hp", bufs=2))
         pp = ctx.enter_context(tc.tile_pool(name="pp", bufs=2))
         p4p = ctx.enter_context(tc.tile_pool(name="p4p", bufs=1))
         p6p = ctx.enter_context(tc.tile_pool(name="p6p", bufs=2))
@@ -61,6 +61,9 @@ def tile_softtreeensemble_pa_kernel(tc, x, W, b, leaf_w, out):
         make_identity(nc, ident16[:])
         brows = const.tile([P, P], BF16, name="brows")
         nc.vector.memset(brows[:], 0.0)
+        warm = const.tile([P, 8], F32, name="warm")
+        nc.vector.memset(warm[:], 0.0)
+        nc.scalar.activation(out=warm[:, 4:5], in_=warm[:, 0:1], func=ACT.Sigmoid)
         bias = const.tile([P, P], F32, name="bias")
         nbias = const.tile([P, P], F32, name="nbias")
         xc = const.tile([P, 1024], U32, name="xc", align_bytes=64)
@@ -72,7 +75,6 @@ def tile_softtreeensemble_pa_kernel(tc, x, W, b, leaf_w, out):
         wg = {}
         wcs = {}
         gts = {}
-        hts = {}
         pt = {}
         p6 = {}
         lraw = {}
@@ -89,13 +91,13 @@ def tile_softtreeensemble_pa_kernel(tc, x, W, b, leaf_w, out):
             )
             raw[u] = r
 
-        def load_leaf(hh):
-            r = rawp.tile([P, 4096], BF16, name="lraw%d" % hh, tag="raw")
+        def load_leaf(piece):
+            r = rawp.tile([P, 4096], BF16, name="lraw%d" % piece, tag="raw")
             nc.sync.dma_start(
-                out=r[:].rearrange("p (j t) -> p j t", j=32),
-                in_=leaf_w[32 * hh : 32 * hh + 32].rearrange("j c t -> c j t"),
+                out=r[:, 0:2048].rearrange("p (j t) -> p j t", j=16),
+                in_=leaf_w[16 * piece : 16 * piece + 16].rearrange("j c t -> c j t"),
             )
-            lraw[hh] = r
+            lraw[piece] = r
 
         def halves(u):
             nn = units[u]["nn"]
@@ -121,14 +123,20 @@ def tile_softtreeensemble_pa_kernel(tc, x, W, b, leaf_w, out):
                     in_=wt[:].rearrange("p (g u m) -> p g m u", g=2, u=2),
                 )
 
-        def quant_w(u):
+        def quant_w(u, half=None):
             if u >= nu:
                 return
-            nn = units[u]["nn"]
-            c = wcp.tile([P, 1024], U32, name="wc%d" % u, tag="wc", align_bytes=64)
-            s = wcp.tile([P, 1024], U8, name="ws%d" % u, tag="ws", align_bytes=64)
-            wcs[u] = (c, s)
-            parts = [(0, 4)] if nn == 4 else [(0, 1), (1, 2)]
+            if u not in wcs:
+                wcs[u] = (
+                    wcp.tile([P, 1024], U32, name="wc%d" % u, tag="wc", align_bytes=64),
+                    wcp.tile([P, 1024], U8, name="ws%d" % u, tag="ws", align_bytes=64),
+                )
+            c, s = wcs[u]
+            if half is None:
+                parts = [(0, 4)]
+            else:
+                es = halves(u)[half]
+                parts = [(es[0], len(es))]
             for e0, ne in parts:
                 nc.vector.quantize_mx(
                     out=c[:, 256 * e0 : 256 * (e0 + ne)].bitcast(FP8X4),
@@ -142,8 +150,6 @@ def tile_softtreeensemble_pa_kernel(tc, x, W, b, leaf_w, out):
             un = units[u]
             if half == 0:
                 gts[u] = gp.tile([P, 2048], F32, name="g%d" % u, tag="g")
-                if un["kind"] == "leaf":
-                    hts[u] = hp.tile([P, 2048], F32, name="h%d" % u, tag="h")
                 if un["kind"] == "top":
                     pt["p1"] = pp.tile([P, 4096], F32, name="p1", tag="p8")
             c, s = wcs[u]
@@ -169,50 +175,49 @@ def tile_softtreeensemble_pa_kernel(tc, x, W, b, leaf_w, out):
                     nc.scalar.activation(out=pt["p1"][:, 512:1024], in_=z[:], func=ACT.Sigmoid, bias=nbias[:, 0:1], scale=-1.0)
                     continue
                 nc.scalar.activation(out=gts[u][:, 512 * e : 512 * e + 512], in_=z[:], func=ACT.Sigmoid, bias=bias[:, n : n + 1], scale=1.0)
-                if un["kind"] == "leaf" and e < 4 - H_ON_VECTOR:
-                    nc.scalar.activation(out=hts[u][:, 512 * e : 512 * e + 512], in_=z[:], func=ACT.Sigmoid, bias=nbias[:, n : n + 1], scale=-1.0)
 
-        def tree_a(u):
+        def mid_views(u, half):
+            un = units[u]
+            nn = 2 if un["kind"] == "top" else 4
+            g0 = 512 if un["kind"] == "top" else 0
+            j0 = 0
+            if half is not None:
+                nn, j0 = 2, 2 * half
+            par = pt[un["par"]][:, 512 * (un["pj"] + j0) : 512 * (un["pj"] + j0 + nn)].rearrange("p (j w) -> p j w", w=512)
+            chv = pt[un["ch"]][:, 1024 * (un["cj"] + j0) : 1024 * (un["cj"] + j0 + nn)].rearrange("p (j b w) -> p j b w", b=2, w=512)
+            gv = gts[u][:, g0 + 512 * j0 : g0 + 512 * (j0 + nn)].rearrange("p (j w) -> p j w", w=512)
+            return par, chv, gv
+
+        def tree_a(u, half=None):
             if u < 0 or u >= nu:
                 return
             un = units[u]
             if un["kind"] == "leaf":
-                par = pt["p5"][:, 512 * un["pj"] : 512 * un["pj"] + 2048].rearrange("p (t c i) -> p c t i", t=4, i=4)
-                if H_ON_VECTOR:
-                    lo = 512 * (4 - H_ON_VECTOR)
-                    nc.vector.tensor_scalar(out=hts[u][:, lo:2048], in0=gts[u][:, lo:2048], scalar1=-1.0, scalar2=1.0, op0=ALU.mult, op1=ALU.add)
+                par = pt["p5"][:, 512 * un["pj"] : 512 * un["pj"] + 2048].rearrange("p (t w) -> p w t", t=4)
                 pg = p6p.tile([P, 4096], BF16, name="p6g%d" % u, tag="p6g", align_bytes=64)
                 p6[u] = pg
-                nc.vector.tensor_tensor(
-                    out=pg[:, 0:2048].rearrange("p (c i t) -> p c t i", i=4, t=4),
-                    in0=par,
-                    in1=gts[u][:].rearrange("p (t c i) -> p c t i", t=4, i=4),
-                    op=ALU.mult,
-                )
-                nc.vector.tensor_tensor(
-                    out=pg[:, 2048:4096].rearrange("p (c i t) -> p c t i", i=4, t=4),
-                    in0=par,
-                    in1=hts[u][:].rearrange("p (t c i) -> p c t i", t=4, i=4),
-                    op=ALU.mult,
-                )
+                for bb in range(2):
+                    nc.vector.scalar_tensor_tensor(
+                        out=pg[:, 2048 * bb : 2048 * bb + 2048].rearrange("p (w t) -> p w t", t=4),
+                        in0=gts[u][:].rearrange("p (t w) -> p w t", t=4),
+                        scalar=(-1.0 if bb == 0 else 1.0),
+                        in1=par,
+                        op0=(ALU.mult if bb == 0 else ALU.subtract),
+                        op1=ALU.mult,
+                    )
                 return
-            nn = 2 if un["kind"] == "top" else 4
-            g0 = 512 if un["kind"] == "top" else 0
-            if un["cj"] == 0:
+            if un["cj"] == 0 and not half:
                 if un["ch"] == "p4":
                     pt["p4"] = p4p.tile([P, 8192], F32, name="p4")
                 else:
                     pt[un["ch"]] = pp.tile([P, 4096], F32, name="%s_%d" % (un["ch"], u), tag="p8")
-            par = pt[un["par"]][:, 512 * un["pj"] : 512 * (un["pj"] + nn)].rearrange("p (j w) -> p j w", w=512)
-            chv = pt[un["ch"]][:, 1024 * un["cj"] : 1024 * (un["cj"] + nn)].rearrange("p (j b w) -> p j b w", b=2, w=512)
-            nc.vector.tensor_tensor(
-                out=chv[:, :, 0, :],
-                in0=par,
-                in1=gts[u][:, g0 : g0 + 512 * nn].rearrange("p (j w) -> p j w", w=512),
-                op=ALU.mult,
-            )
+            par, chv, gv = mid_views(u, half)
+            if un["ch"] == "p5":
+                nc.vector.scalar_tensor_tensor(out=chv[:, :, 0, :], in0=gv, scalar=-1.0, in1=par, op0=ALU.mult, op1=ALU.mult)
+                return
+            nc.vector.tensor_tensor(out=chv[:, :, 0, :], in0=par, in1=gv, op=ALU.mult)
 
-        def tree_b(u):
+        def tree_b(u, half=None):
             if u < 0 or u >= nu:
                 return
             un = units[u]
@@ -227,17 +232,37 @@ def tile_softtreeensemble_pa_kernel(tc, x, W, b, leaf_w, out):
                     )
                 p6[u] = (c, s)
                 return
-            nn = 2 if un["kind"] == "top" else 4
-            par = pt[un["par"]][:, 512 * un["pj"] : 512 * (un["pj"] + nn)].rearrange("p (j w) -> p j w", w=512)
-            chv = pt[un["ch"]][:, 1024 * un["cj"] : 1024 * (un["cj"] + nn)].rearrange("p (j b w) -> p j b w", b=2, w=512)
+            par, chv, gv = mid_views(u, half)
+            if un["ch"] == "p5":
+                nc.vector.scalar_tensor_tensor(out=chv[:, :, 1, :], in0=gv, scalar=1.0, in1=par, op0=ALU.subtract, op1=ALU.mult)
+                return
             nc.vector.tensor_tensor(out=chv[:, :, 1, :], in0=par, in1=chv[:, :, 0, :], op=ALU.subtract)
 
         o_ps = ps_o.tile([P, 512], F32, name="o_ps")
+        o_t = const.tile([P, 2048], F32, name="o_t")
+        last = {}
 
         def second(u):
             if u < 0 or u >= nu or units[u]["kind"] != "leaf":
                 return
             c, s = p6[u]
+            if u == nu - 1:
+                for bb in range(2):
+                    q = units[u]["q0"] + bb
+                    o2 = ps_t.tile([P, 512], F32, name="o2_%d" % bb, tag="wt")
+                    last[bb] = o2
+                    for k in range(4):
+                        cols = slice(512 * bb + 128 * k, 512 * bb + 128 * k + 128)
+                        nc.tensor.matmul_mx(
+                            out=o2[:, 128 * k : 128 * k + 128],
+                            lhsT=c[:, cols].bitcast(FP8X4),
+                            lhsT_scale=s[:, cols],
+                            rhs=lwc[:, 128 * q : 128 * q + 128].bitcast(FP8X4),
+                            rhs_scale=lws[:, 128 * q : 128 * q + 128],
+                            start=True,
+                            stop=True,
+                        )
+                return
             for bb in range(2):
                 q = units[u]["q0"] + bb
                 nc.tensor.matmul_mx(
@@ -247,11 +272,16 @@ def tile_softtreeensemble_pa_kernel(tc, x, W, b, leaf_w, out):
                     rhs=c[:, 512 * bb : 512 * bb + 512].bitcast(FP8X4),
                     rhs_scale=s[:, 512 * bb : 512 * bb + 512],
                     start=(q == 0),
-                    stop=(q == 15),
+                    stop=(q == 13),
                 )
+            if u == nu - 2:
+                nc.scalar.copy(out=o_t[:, 0:512], in_=o_ps[:])
+                o_b = ps_t.tile([P, 512], F32, name="o_b", tag="wt")
+                for k in range(4):
+                    nc.tensor.transpose(o_b[:, 128 * k : 128 * k + 128], o_t[:, 128 * k : 128 * k + 128], ident32[:])
+                nc.scalar.copy(out=o_t[:, 512:1024], in_=o_b[:])
 
         def leaf_tc(piece):
-            hh = piece // 2
             lg = lgp.tile([P, 2048], BF16, name="lg%d" % piece, tag="lg", align_bytes=64)
             lgs[piece] = lg
             banks = []
@@ -260,8 +290,8 @@ def tile_softtreeensemble_pa_kernel(tc, x, W, b, leaf_w, out):
                 bank = ps_t.tile([P, 1024], BF16, name="lt%d" % a, tag="wt")
                 for bb in range(2):
                     for t in range(4):
-                        jl = 8 * a + 2 * t + bb - 32 * hh
-                        nc.tensor.transpose(bank[:, (4 * bb + t) * 128 : (4 * bb + t) * 128 + 128], lraw[hh][:, 128 * jl : 128 * jl + 128], ident16[:])
+                        jl = 8 * a + 2 * t + bb - 16 * piece
+                        nc.tensor.transpose(bank[:, (4 * bb + t) * 128 : (4 * bb + t) * 128 + 128], lraw[piece][:, 128 * jl : 128 * jl + 128], ident16[:])
                 banks.append(bank)
             for k in range(2):
                 nc.scalar.copy(
@@ -303,43 +333,64 @@ def tile_softtreeensemble_pa_kernel(tc, x, W, b, leaf_w, out):
                     nc.vector.tensor_copy(out=dst, in_=srcv)
                 else:
                     nc.scalar.copy(out=dst, in_=srcv)
+        nc.vector.quantize_mx(out=xc[:].bitcast(FP8X4), scales=xs[:], in_=xg[:].bitcast(BF16))
         bt = ps_t.tile([P, 1024], BF16, name="bt", tag="wt")
         nc.tensor.transpose(bt[:, 0:128], brows[:], ident16[:])
         nc.vector.tensor_copy(out=bias[:], in_=bt[:, 0:128])
         nc.vector.tensor_scalar(out=nbias[:], in0=bias[:], scalar1=-1.0, scalar2=0.0, op0=ALU.mult, op1=ALU.add)
-        nc.vector.quantize_mx(out=xc[:].bitcast(FP8X4), scales=xs[:], in_=xg[:].bitcast(BF16))
 
-        for u in range(2):
-            for half in range(2):
-                transpose_copy_w(u, half)
-        quant_w(0)
+        transpose_copy_w(0, 0)
+        transpose_copy_w(0, 1)
+        quant_w(0, 0)
+        quant_w(0, 1)
+        gates(0, 0)
+        transpose_copy_w(1, 0)
+        transpose_copy_w(1, 1)
+        load_w(3)
+        gates(0, 1)
+        transpose_copy_w(2, 0)
+        transpose_copy_w(2, 1)
+        quant_w(1, 0)
+        quant_w(1, 1)
+        load_w(4)
+        gates(1, 0)
+        transpose_copy_w(3, 0)
+        gates(1, 1)
+        transpose_copy_w(3, 1)
+        tree_a(0)
+        quant_w(2)
+        tree_b(0)
+        load_w(5)
+        gates(2, 0)
+        transpose_copy_w(4, 0)
+        gates(2, 1)
+        transpose_copy_w(4, 1)
+        tree_a(1, 0)
+        tree_a(1, 1)
+        quant_w(3)
+        tree_b(1, 0)
+        tree_b(1, 1)
 
-        for it in range(nu + 2):
-            if it == 0:
-                load_leaf(0)
-            if it == 2:
-                load_leaf(1)
+        for it in range(3, nu + 2):
+            if it in LEAF_LOAD_AT:
+                load_leaf(LEAF_LOAD_AT.index(it))
             load_w(it + 3)
             for half in range(2):
                 gates(it, half)
                 if half == 0:
                     second(it - 2)
                 transpose_copy_w(it + 2, half)
-            if 1 <= it <= 4:
-                leaf_tc(it - 1)
+            if it in LEAF_WORK_AT:
+                leaf_tc(LEAF_WORK_AT.index(it))
             tree_a(it - 1)
             quant_w(it + 1)
-            if 2 <= it <= 5:
-                leaf_q(it - 2)
+            if it - 1 in LEAF_WORK_AT:
+                leaf_q(LEAF_WORK_AT.index(it - 1))
             tree_b(it - 1)
 
-        o_t = hp.tile([P, 2048], F32, name="o_t", tag="h")
-        nc.vector.tensor_copy(out=o_t[:, 0:512], in_=o_ps[:])
-        o_b = ps_t.tile([P, 512], F32, name="o_b", tag="wt")
-        for k in range(4):
-            nc.tensor.transpose(o_b[:, 128 * k : 128 * k + 128], o_t[:, 128 * k : 128 * k + 128], ident32[:])
-        nc.vector.tensor_copy(out=o_t[:, 512:1024], in_=o_b[:])
+        nc.vector.tensor_tensor(out=o_t[:, 1024:1536], in0=o_t[:, 512:1024], in1=last[0][:], op=ALU.add)
+        nc.vector.tensor_tensor(out=o_t[:, 1536:2048], in0=o_t[:, 1024:1536], in1=last[1][:], op=ALU.add)
         nc.sync.dma_start(
             out=out.rearrange("(k p) c -> p k c", p=P),
-            in_=o_t[:, 512:1024].rearrange("p (k c) -> p k c", k=4),
+            in_=o_t[:, 1536:2048].rearrange("p (k c) -> p k c", k=4),
         )

@@ -17,6 +17,7 @@ NI, NL = 63, 64
 FLOPS = 2 * B * D * NI * T + 2 * B * NL * T * LD
 
 PINNED = False
+H_ON_VECTOR = 0
 LEAF_LOAD_AT = [3, 5, 8, 11]
 LEAF_WORK_AT = [4, 7, 10, 13]
 
@@ -46,6 +47,7 @@ def tile_softtreeensemble_pa_kernel(tc, x, W, b, leaf_w, out):
         lgp = ctx.enter_context(tc.tile_pool(name="lgp", bufs=2))
         wcp = ctx.enter_context(tc.tile_pool(name="wcp", bufs=2))
         gp = ctx.enter_context(tc.tile_pool(name="gp", bufs=3))
+        hp = ctx.enter_context(tc.tile_pool(name="hp", bufs=2))
         pp = ctx.enter_context(tc.tile_pool(name="pp", bufs=2))
         p4p = ctx.enter_context(tc.tile_pool(name="p4p", bufs=1))
         p6p = ctx.enter_context(tc.tile_pool(name="p6p", bufs=2))
@@ -75,6 +77,7 @@ def tile_softtreeensemble_pa_kernel(tc, x, W, b, leaf_w, out):
         wg = {}
         wcs = {}
         gts = {}
+        hts = {}
         pt = {}
         p6 = {}
         lraw = {}
@@ -150,6 +153,8 @@ def tile_softtreeensemble_pa_kernel(tc, x, W, b, leaf_w, out):
             un = units[u]
             if half == 0:
                 gts[u] = gp.tile([P, 2048], F32, name="g%d" % u, tag="g")
+                if un["kind"] == "leaf":
+                    hts[u] = hp.tile([P, 2048], F32, name="h%d" % u, tag="h")
                 if un["kind"] == "top":
                     pt["p1"] = pp.tile([P, 4096], F32, name="p1", tag="p8")
             c, s = wcs[u]
@@ -175,6 +180,8 @@ def tile_softtreeensemble_pa_kernel(tc, x, W, b, leaf_w, out):
                     nc.scalar.activation(out=pt["p1"][:, 512:1024], in_=z[:], func=ACT.Sigmoid, bias=nbias[:, 0:1], scale=-1.0)
                     continue
                 nc.scalar.activation(out=gts[u][:, 512 * e : 512 * e + 512], in_=z[:], func=ACT.Sigmoid, bias=bias[:, n : n + 1], scale=1.0)
+                if un["kind"] == "leaf" and e < 4 - H_ON_VECTOR:
+                    nc.scalar.activation(out=hts[u][:, 512 * e : 512 * e + 512], in_=z[:], func=ACT.Sigmoid, bias=nbias[:, n : n + 1], scale=-1.0)
 
         def mid_views(u, half):
             un = units[u]
@@ -193,18 +200,24 @@ def tile_softtreeensemble_pa_kernel(tc, x, W, b, leaf_w, out):
                 return
             un = units[u]
             if un["kind"] == "leaf":
-                par = pt["p5"][:, 512 * un["pj"] : 512 * un["pj"] + 2048].rearrange("p (t w) -> p w t", t=4)
+                par = pt["p5"][:, 512 * un["pj"] : 512 * un["pj"] + 2048].rearrange("p (t c i) -> p c t i", t=4, i=4)
+                if H_ON_VECTOR:
+                    lo = 512 * (4 - H_ON_VECTOR)
+                    nc.vector.tensor_scalar(out=hts[u][:, lo:2048], in0=gts[u][:, lo:2048], scalar1=-1.0, scalar2=1.0, op0=ALU.mult, op1=ALU.add)
                 pg = p6p.tile([P, 4096], BF16, name="p6g%d" % u, tag="p6g", align_bytes=64)
                 p6[u] = pg
-                for bb in range(2):
-                    nc.vector.scalar_tensor_tensor(
-                        out=pg[:, 2048 * bb : 2048 * bb + 2048].rearrange("p (w t) -> p w t", t=4),
-                        in0=gts[u][:].rearrange("p (t w) -> p w t", t=4),
-                        scalar=(-1.0 if bb == 0 else 1.0),
-                        in1=par,
-                        op0=(ALU.mult if bb == 0 else ALU.subtract),
-                        op1=ALU.mult,
-                    )
+                nc.vector.tensor_tensor(
+                    out=pg[:, 0:2048].rearrange("p (c i t) -> p c t i", i=4, t=4),
+                    in0=par,
+                    in1=gts[u][:].rearrange("p (t c i) -> p c t i", t=4, i=4),
+                    op=ALU.mult,
+                )
+                nc.vector.tensor_tensor(
+                    out=pg[:, 2048:4096].rearrange("p (c i t) -> p c t i", i=4, t=4),
+                    in0=par,
+                    in1=hts[u][:].rearrange("p (t c i) -> p c t i", t=4, i=4),
+                    op=ALU.mult,
+                )
                 return
             if un["cj"] == 0 and not half:
                 if un["ch"] == "p4":
@@ -212,9 +225,6 @@ def tile_softtreeensemble_pa_kernel(tc, x, W, b, leaf_w, out):
                 else:
                     pt[un["ch"]] = pp.tile([P, 4096], F32, name="%s_%d" % (un["ch"], u), tag="p8")
             par, chv, gv = mid_views(u, half)
-            if un["ch"] == "p5":
-                nc.vector.scalar_tensor_tensor(out=chv[:, :, 0, :], in0=gv, scalar=-1.0, in1=par, op0=ALU.mult, op1=ALU.mult)
-                return
             nc.vector.tensor_tensor(out=chv[:, :, 0, :], in0=par, in1=gv, op=ALU.mult)
 
         def tree_b(u, half=None):
@@ -233,9 +243,6 @@ def tile_softtreeensemble_pa_kernel(tc, x, W, b, leaf_w, out):
                 p6[u] = (c, s)
                 return
             par, chv, gv = mid_views(u, half)
-            if un["ch"] == "p5":
-                nc.vector.scalar_tensor_tensor(out=chv[:, :, 1, :], in0=gv, scalar=1.0, in1=par, op0=ALU.subtract, op1=ALU.mult)
-                return
             nc.vector.tensor_tensor(out=chv[:, :, 1, :], in0=par, in1=chv[:, :, 0, :], op=ALU.subtract)
 
         o_ps = ps_o.tile([P, 512], F32, name="o_ps")

@@ -17,7 +17,7 @@ NI, NL = 63, 64
 FLOPS = 2 * B * D * NI * T + 2 * B * NL * T * LD
 
 PINNED = False
-H_ON_VECTOR = 0
+H_ON_VECTOR = 1
 LEAF_LOAD_AT = [3, 5, 8, 11]
 LEAF_WORK_AT = [4, 7, 10, 13]
 

@@ -17,7 +17,7 @@ NI, NL = 63, 64
 FLOPS = 2 * B * D * NI * T + 2 * B * NL * T * LD
 
 PINNED = False
-H_ON_VECTOR = 1
+H_ON_VECTOR = 0
 LEAF_LOAD_AT = [3, 5, 8, 11]
 LEAF_WORK_AT = [4, 7, 10, 13]
 
@@ -207,13 +207,13 @@ def tile_softtreeensemble_pa_kernel(tc, x, W, b, leaf_w, out):
                 pg = p6p.tile([P, 4096], BF16, name="p6g%d" % u, tag="p6g", align_bytes=64)
                 p6[u] = pg
                 nc.vector.tensor_tensor(
-                    out=pg[:, 0:2048].rearrange("p (c i t) -> p c t i", i=4, t=4),
+                    out=pg[:, 0:2048].rearrange("p (i c t) -> p c t i", i=4, t=4),
                     in0=par,
                     in1=gts[u][:].rearrange("p (t c i) -> p c t i", t=4, i=4),
                     op=ALU.mult,
                 )
                 nc.vector.tensor_tensor(
-                    out=pg[:, 2048:4096].rearrange("p (c i t) -> p c t i", i=4, t=4),
+                    out=pg[:, 2048:4096].rearrange("p (i c t) -> p c t i", i=4, t=4),
                     in0=par,
                     in1=hts[u][:].rearrange("p (t c i) -> p c t i", t=4, i=4),
                     op=ALU.mult,
@@ -398,6 +398,6 @@ def tile_softtreeensemble_pa_kernel(tc, x, W, b, leaf_w, out):
         nc.vector.tensor_tensor(out=o_t[:, 1024:1536], in0=o_t[:, 512:1024], in1=last[0][:], op=ALU.add)
         nc.vector.tensor_tensor(out=o_t[:, 1536:2048], in0=o_t[:, 1024:1536], in1=last[1][:], op=ALU.add)
         nc.sync.dma_start(
-            out=out.rearrange("(k p) c -> p k c", p=P),
+            out=out.rearrange("(p k) c -> p k c", k=4),
             in_=o_t[:, 1536:2048].rearrange("p (k c) -> p k c", k=4),
         )

@@ -88,10 +88,11 @@ def tile_softtreeensemble_pa_kernel(tc, x, W, b, leaf_w, out):
                 return
             n0, nn = units[u]["n0"], units[u]["nn"]
             r = rawp.tile([P, 4096], BF16, name="raw%d" % u, tag="raw")
-            nc.sync.dma_start(
-                out=r[:, : nn * 1024].rearrange("p (n d) -> p n d", n=nn),
-                in_=W[n0 : n0 + nn].rearrange("n t d -> t n d"),
-            )
+            for e0, ne in ([(0, 1), (1, 2)] if u == 0 else [(0, nn)]):
+                nc.sync.dma_start(
+                    out=r[:, e0 * 1024 : (e0 + ne) * 1024].rearrange("p (n d) -> p n d", n=ne),
+                    in_=W[n0 + e0 : n0 + e0 + ne].rearrange("n t d -> t n d"),
+                )
             raw[u] = r
 
         def load_leaf(piece):
@@ -180,8 +181,10 @@ def tile_softtreeensemble_pa_kernel(tc, x, W, b, leaf_w, out):
                     nc.scalar.activation(out=pt["p1"][:, 512:1024], in_=z[:], func=ACT.Sigmoid, bias=nbias[:, 0:1], scale=-1.0)
                     continue
                 nc.scalar.activation(out=gts[u][:, 512 * e : 512 * e + 512], in_=z[:], func=ACT.Sigmoid, bias=bias[:, n : n + 1], scale=1.0)
-                if un["kind"] == "leaf" and e < 4 - H_ON_VECTOR:
-                    nc.scalar.activation(out=hts[u][:, 512 * e : 512 * e + 512], in_=z[:], func=ACT.Sigmoid, bias=nbias[:, n : n + 1], scale=-1.0)
+
+        def one_minus(u):
+            if u < nu and units[u]["kind"] == "leaf":
+                nc.scalar.activation(out=hts[u][:], in_=gts[u][:], func=ACT.Copy, bias=1.0, scale=-1.0)
 
         def mid_views(u, half):
             un = units[u]
@@ -207,13 +210,13 @@ def tile_softtreeensemble_pa_kernel(tc, x, W, b, leaf_w, out):
                 pg = p6p.tile([P, 4096], BF16, name="p6g%d" % u, tag="p6g", align_bytes=64)
                 p6[u] = pg
                 nc.vector.tensor_tensor(
-                    out=pg[:, 0:2048].rearrange("p (i c t) -> p c t i", i=4, t=4),
+                    out=pg[:, 0:2048].rearrange("p (c i t) -> p c t i", i=4, t=4),
                     in0=par,
                     in1=gts[u][:].rearrange("p (t c i) -> p c t i", t=4, i=4),
                     op=ALU.mult,
                 )
                 nc.vector.tensor_tensor(
-                    out=pg[:, 2048:4096].rearrange("p (i c t) -> p c t i", i=4, t=4),
+                    out=pg[:, 2048:4096].rearrange("p (c i t) -> p c t i", i=4, t=4),
                     in0=par,
                     in1=hts[u][:].rearrange("p (t c i) -> p c t i", t=4, i=4),
                     op=ALU.mult,
@@ -314,7 +317,7 @@ def tile_softtreeensemble_pa_kernel(tc, x, W, b, leaf_w, out):
             )
 
         xraw = rawp.tile([P, 4096], BF16, name="xraw", tag="raw")
-        xv = x.rearrange("(k p) d -> p k d", p=P)
+        xv = x.rearrange("(p k) d -> p k d", k=4)
         for kk in range(2):
             nc.sync.dma_start(
                 out=xraw[:, 2048 * kk : 2048 * kk + 2048].rearrange("p (k d) -> p k d", k=2),
@@ -386,11 +389,17 @@ def tile_softtreeensemble_pa_kernel(tc, x, W, b, leaf_w, out):
                 gates(it, half)
                 if half == 0:
                     second(it - 2)
+                else:
+                    one_minus(it)
                 transpose_copy_w(it + 2, half)
             if it in LEAF_WORK_AT:
                 leaf_tc(LEAF_WORK_AT.index(it))
+            leaf_unit = it - 1 < nu and units[it - 1]["kind"] == "leaf"
+            if leaf_unit:
+                quant_w(it + 1)
             tree_a(it - 1)
-            quant_w(it + 1)
+            if not leaf_unit:
+                quant_w(it + 1)
             if it - 1 in LEAF_WORK_AT:
                 leaf_q(LEAF_WORK_AT.index(it - 1))
             tree_b(it - 1)

@@ -18,6 +18,7 @@ FLOPS = 2 * B * D * NI * T + 2 * B * NL * T * LD
 
 PINNED = False
 H_ON_VECTOR = 0
+WARM_FIRST = 5
 LEAF_LOAD_AT = [3, 5, 8, 11]
 LEAF_WORK_AT = [4, 7, 10, 13]
 
@@ -57,6 +58,15 @@ def tile_softtreeensemble_pa_kernel(tc, x, W, b, leaf_w, out):
         if PINNED:
             ctx.enter_context(tc.manual_schedule())
 
+        dz = const.tile([P, 512], BF16, name="dz")
+        nc.vector.memset(dz[:], 0.0)
+        o_ps = ps_o.tile([P, 512], F32, name="o_ps")
+
+        def warm_pe(n):
+            for r in range(n):
+                nc.tensor.matmul(out=o_ps[:], lhsT=dz[:, 0:128], rhs=dz[:], start=True, stop=True)
+
+        warm_pe(WARM_FIRST)
         ident32 = const.tile([P, P], F32, name="ident32")
         make_identity(nc, ident32[:])
         ident16 = const.tile([P, P], BF16, name="ident16")
@@ -88,7 +98,7 @@ def tile_softtreeensemble_pa_kernel(tc, x, W, b, leaf_w, out):
                 return
             n0, nn = units[u]["n0"], units[u]["nn"]
             r = rawp.tile([P, 4096], BF16, name="raw%d" % u, tag="raw")
-            for e0, ne in ([(0, 1), (1, 2)] if u == 0 else [(0, nn)]):
+            for e0, ne in ([(0, 1), (1, 2)] if u == 0 else [(0, 2), (2, 2)] if u == 1 else [(0, nn)]):
                 nc.sync.dma_start(
                     out=r[:, e0 * 1024 : (e0 + ne) * 1024].rearrange("p (n d) -> p n d", n=ne),
                     in_=W[n0 + e0 : n0 + e0 + ne].rearrange("n t d -> t n d"),
@@ -121,6 +131,8 @@ def tile_softtreeensemble_pa_kernel(tc, x, W, b, leaf_w, out):
                 for s in range(4):
                     nc.tensor.transpose(wt[:, 128 * s : 128 * s + 128], rw[:, 512 * e + 128 * s : 512 * e + 128 * s + 128], ident32[:])
                 banks.append((e, wt))
+            if u == 0:
+                warm_pe(1)
             for e, wt in banks:
                 nc.scalar.copy(
                     out=wg[u][:, 512 * e : 512 * e + 512].rearrange("p (g m u) -> p g m u", g=2, u=2),
@@ -248,7 +260,6 @@ def tile_softtreeensemble_pa_kernel(tc, x, W, b, leaf_w, out):
             par, chv, gv = mid_views(u, half)
             nc.vector.tensor_tensor(out=chv[:, :, 1, :], in0=par, in1=chv[:, :, 0, :], op=ALU.subtract)
 
-        o_ps = ps_o.tile([P, 512], F32, name="o_ps")
         o_t = const.tile([P, 2048], F32, name="o_t")
         last = {}
 
@@ -337,6 +348,8 @@ def tile_softtreeensemble_pa_kernel(tc, x, W, b, leaf_w, out):
                     for u2 in range(2):
                         src = 512 * (2 * kk + k2) + 256 * g + 128 * u2
                         nc.tensor.transpose(bank[:, (2 * k2 + u2) * 128 : (2 * k2 + u2) * 128 + 128], xw[:, src : src + 128], ident32[:])
+                if g == 1:
+                    warm_pe(1)
                 dst = xg[:, 1024 * g + 512 * kk : 1024 * g + 512 * kk + 512].rearrange("p (k i u) -> p k i u", k=2, u=2)
                 srcv = bank[:].rearrange("p (k u i) -> p k i u", k=2, u=2)
                 if g == 0:

@@ -16,7 +16,10 @@ B, D, T, LD = 512, 1024, 128, 128
 NI, NL = 63, 64
 FLOPS = 2 * B * D * NI * T + 2 * B * NL * T * LD
 
-PINNED = False
+PINNED = True
+COPY_ON_V = {(1,1),(1,3)}
+SL = 3
+HV = {5, 8}
 H_ON_VECTOR = 0
 WARM_FIRST = 5
 LEAF_LOAD_AT = [3, 5, 8, 11]
@@ -52,6 +55,7 @@ def tile_softtreeensemble_pa_kernel(tc, x, W, b, leaf_w, out):
         pp = ctx.enter_context(tc.tile_pool(name="pp", bufs=2))
         p4p = ctx.enter_context(tc.tile_pool(name="p4p", bufs=1))
         p6p = ctx.enter_context(tc.tile_pool(name="p6p", bufs=2))
+        p6q = ctx.enter_context(tc.tile_pool(name="p6q", bufs=3))
         ps_t = ctx.enter_context(tc.psum_pool(name="ps_t", bufs=4))
         ps_z = ctx.enter_context(tc.psum_pool(name="ps_z", bufs=3))
         ps_o = ctx.enter_context(tc.psum_pool(name="ps_o", bufs=1))
@@ -119,27 +123,33 @@ def tile_softtreeensemble_pa_kernel(tc, x, W, b, leaf_w, out):
                 return [[0], [1, 2]]
             return [[0, 1], [2, 3]]
 
+        wts = {}
+
+        def tr_w(u, e):
+            rw = raw[u][:].bitcast(F32)
+            wt = ps_t.tile([P, 512], F32, name="wt%d_%d" % (u, e), tag="wt")
+            for s in range(4):
+                nc.tensor.transpose(wt[:, 128 * s : 128 * s + 128], rw[:, 512 * e + 128 * s : 512 * e + 128 * s + 128], ident32[:])
+            wts[u, e] = wt
+
+        def cp_w(u, e):
+            if u not in wg:
+                wg[u] = grpp.tile([P, 2048], F32, name="wg%d" % u, tag="grp", align_bytes=64)
+            copy = nc.vector.tensor_copy if (u, e) in COPY_ON_V else nc.scalar.copy
+            copy(
+                out=wg[u][:, 512 * e : 512 * e + 512].rearrange("p (g m u) -> p g m u", g=2, u=2),
+                in_=wts[u, e][:].rearrange("p (g u m) -> p g m u", g=2, u=2),
+            )
+
         def transpose_copy_w(u, half):
             if u >= nu:
                 return
-            if half == 0:
-                wg[u] = grpp.tile([P, 2048], F32, name="wg%d" % u, tag="grp", align_bytes=64)
-            rw = raw[u][:].bitcast(F32)
-            banks = []
             for e in halves(u)[half]:
-                wt = ps_t.tile([P, 512], F32, name="wt%d_%d" % (u, e), tag="wt")
-                for s in range(4):
-                    nc.tensor.transpose(wt[:, 128 * s : 128 * s + 128], rw[:, 512 * e + 128 * s : 512 * e + 128 * s + 128], ident32[:])
-                banks.append((e, wt))
-            if u == 0:
-                warm_pe(1)
-            for e, wt in banks:
-                nc.scalar.copy(
-                    out=wg[u][:, 512 * e : 512 * e + 512].rearrange("p (g m u) -> p g m u", g=2, u=2),
-                    in_=wt[:].rearrange("p (g u m) -> p g m u", g=2, u=2),
-                )
+                tr_w(u, e)
+            for e in halves(u)[half]:
+                cp_w(u, e)
 
-        def quant_w(u, half=None):
+        def quant_w(u, half=None, nodes=None):
             if u >= nu:
                 return
             if u not in wcs:
@@ -148,7 +158,9 @@ def tile_softtreeensemble_pa_kernel(tc, x, W, b, leaf_w, out):
                     wcp.tile([P, 1024], U8, name="ws%d" % u, tag="ws", align_bytes=64),
                 )
             c, s = wcs[u]
-            if half is None:
+            if nodes is not None:
+                parts = [nodes]
+            elif half is None:
                 parts = [(0, 4)]
             else:
                 es = halves(u)[half]
@@ -163,16 +175,23 @@ def tile_softtreeensemble_pa_kernel(tc, x, W, b, leaf_w, out):
         def gates(u, half):
             if u >= nu:
                 return
+            for e in halves(u)[half]:
+                mx_z(u, e)
+            for e in halves(u)[half]:
+                sig(u, e)
+
+        zts = {}
+
+        def mx_z(u, e):
             un = units[u]
-            if half == 0:
+            if u not in gts:
                 gts[u] = gp.tile([P, 2048], F32, name="g%d" % u, tag="g")
                 if un["kind"] == "leaf":
                     hts[u] = hp.tile([P, 2048], F32, name="h%d" % u, tag="h")
                 if un["kind"] == "top":
                     pt["p1"] = pp.tile([P, 4096], F32, name="p1", tag="p8")
             c, s = wcs[u]
-            zs = []
-            for e in halves(u)[half]:
+            if True:
                 z = ps_z.tile([P, 512], F32, name="z%d_%d" % (u, e), tag="z")
                 for g in range(2):
                     cols = slice(256 * e + 128 * g, 256 * e + 128 * g + 128)
@@ -185,17 +204,20 @@ def tile_softtreeensemble_pa_kernel(tc, x, W, b, leaf_w, out):
                         start=(g == 0),
                         stop=(g == 1),
                     )
-                zs.append((e, z))
-            for e, z in zs:
-                n = un["n0"] + e
-                if n == 0:
-                    nc.scalar.activation(out=pt["p1"][:, 0:512], in_=z[:], func=ACT.Sigmoid, bias=bias[:, 0:1], scale=1.0)
-                    nc.scalar.activation(out=pt["p1"][:, 512:1024], in_=z[:], func=ACT.Sigmoid, bias=nbias[:, 0:1], scale=-1.0)
-                    continue
+                zts[u, e] = z
+
+        def sig(u, e):
+            n = units[u]["n0"] + e
+            z = zts[u, e]
+            if n == 0:
+                nc.scalar.activation(out=pt["p1"][:, 0:512], in_=z[:], func=ACT.Sigmoid, bias=bias[:, 0:1], scale=1.0)
+                nc.vector.tensor_scalar(out=pt["p1"][:, 512:1024], in0=pt["p1"][:, 0:512], scalar1=-1.0, scalar2=1.0, op0=ALU.mult, op1=ALU.add)
+                return
+            if True:
                 nc.scalar.activation(out=gts[u][:, 512 * e : 512 * e + 512], in_=z[:], func=ACT.Sigmoid, bias=bias[:, n : n + 1], scale=1.0)
 
         def one_minus(u):
-            if u < nu and units[u]["kind"] == "leaf":
+            if u < nu and units[u]["kind"] == "leaf" and u not in HV:
                 nc.scalar.activation(out=hts[u][:], in_=gts[u][:], func=ACT.Copy, bias=1.0, scale=-1.0)
 
         def mid_views(u, half):
@@ -210,15 +232,28 @@ def tile_softtreeensemble_pa_kernel(tc, x, W, b, leaf_w, out):
             gv = gts[u][:, g0 + 512 * j0 : g0 + 512 * (j0 + nn)].rearrange("p (j w) -> p j w", w=512)
             return par, chv, gv
 
+        p6c = {}
+
+        def quant_p6(u, bb):
+            if bb == 0:
+                c = p6q.tile([P, 1024], U32, name="p6c%d" % u, tag="p6c", align_bytes=64)
+                s = p6q.tile([P, 1024], U8, name="p6s%d" % u, tag="p6s", align_bytes=64)
+                p6c[u] = (c, s)
+            c, s = p6c[u]
+            nc.vector.quantize_mx(
+                out=c[:, 512 * bb : 512 * bb + 512].bitcast(FP8X4),
+                scales=s[:, 512 * bb : 512 * bb + 512],
+                in_=p6[u][:, 2048 * bb : 2048 * bb + 2048],
+            )
+
         def tree_a(u, half=None):
             if u < 0 or u >= nu:
                 return
             un = units[u]
             if un["kind"] == "leaf":
                 par = pt["p5"][:, 512 * un["pj"] : 512 * un["pj"] + 2048].rearrange("p (t c i) -> p c t i", t=4, i=4)
-                if H_ON_VECTOR:
-                    lo = 512 * (4 - H_ON_VECTOR)
-                    nc.vector.tensor_scalar(out=hts[u][:, lo:2048], in0=gts[u][:, lo:2048], scalar1=-1.0, scalar2=1.0, op0=ALU.mult, op1=ALU.add)
+                if u in HV:
+                    nc.vector.tensor_scalar(out=hts[u][:], in0=gts[u][:], scalar1=-1.0, scalar2=1.0, op0=ALU.mult, op1=ALU.add)
                 pg = p6p.tile([P, 4096], BF16, name="p6g%d" % u, tag="p6g", align_bytes=64)
                 p6[u] = pg
                 nc.vector.tensor_tensor(
@@ -227,6 +262,8 @@ def tile_softtreeensemble_pa_kernel(tc, x, W, b, leaf_w, out):
                     in1=gts[u][:].rearrange("p (t c i) -> p c t i", t=4, i=4),
                     op=ALU.mult,
                 )
+                if u == nu - 1:
+                    quant_p6(u, 0)
                 nc.vector.tensor_tensor(
                     out=pg[:, 2048:4096].rearrange("p (c i t) -> p c t i", i=4, t=4),
                     in0=par,
@@ -247,15 +284,9 @@ def tile_softtreeensemble_pa_kernel(tc, x, W, b, leaf_w, out):
                 return
             un = units[u]
             if un["kind"] == "leaf":
-                c = p6p.tile([P, 1024], U32, name="p6c%d" % u, tag="p6c", align_bytes=64)
-                s = p6p.tile([P, 1024], U8, name="p6s%d" % u, tag="p6s", align_bytes=64)
-                for bb in range(2):
-                    nc.vector.quantize_mx(
-                        out=c[:, 512 * bb : 512 * bb + 512].bitcast(FP8X4),
-                        scales=s[:, 512 * bb : 512 * bb + 512],
-                        in_=p6[u][:, 2048 * bb : 2048 * bb + 2048],
-                    )
-                p6[u] = (c, s)
+                if u != nu - 1:
+                    quant_p6(u, 0)
+                quant_p6(u, 1)
                 return
             par, chv, gv = mid_views(u, half)
             nc.vector.tensor_tensor(out=chv[:, :, 1, :], in0=par, in1=chv[:, :, 0, :], op=ALU.subtract)
@@ -266,12 +297,12 @@ def tile_softtreeensemble_pa_kernel(tc, x, W, b, leaf_w, out):
         def second(u):
             if u < 0 or u >= nu or units[u]["kind"] != "leaf":
                 return
-            c, s = p6[u]
-            if u == nu - 1:
-                for bb in range(2):
-                    q = units[u]["q0"] + bb
-                    o2 = ps_t.tile([P, 512], F32, name="o2_%d" % bb, tag="wt")
-                    last[bb] = o2
+            c, s = p6c[u]
+            for bb in range(2):
+                q = units[u]["q0"] + bb
+                if q == 15:
+                    o2 = ps_t.tile([P, 512], F32, name="o2", tag="wt")
+                    last[0] = o2
                     for k in range(4):
                         cols = slice(512 * bb + 128 * k, 512 * bb + 128 * k + 128)
                         nc.tensor.matmul_mx(
@@ -283,9 +314,7 @@ def tile_softtreeensemble_pa_kernel(tc, x, W, b, leaf_w, out):
                             start=True,
                             stop=True,
                         )
-                return
-            for bb in range(2):
-                q = units[u]["q0"] + bb
+                    continue
                 nc.tensor.matmul_mx(
                     out=o_ps[:],
                     lhsT=lwc[:, 128 * q : 128 * q + 128].bitcast(FP8X4),
@@ -293,14 +322,14 @@ def tile_softtreeensemble_pa_kernel(tc, x, W, b, leaf_w, out):
                     rhs=c[:, 512 * bb : 512 * bb + 512].bitcast(FP8X4),
                     rhs_scale=s[:, 512 * bb : 512 * bb + 512],
                     start=(q == 0),
-                    stop=(q == 13),
+                    stop=(q == 14),
                 )
-            if u == nu - 2:
-                nc.scalar.copy(out=o_t[:, 0:512], in_=o_ps[:])
-                o_b = ps_t.tile([P, 512], F32, name="o_b", tag="wt")
-                for k in range(4):
-                    nc.tensor.transpose(o_b[:, 128 * k : 128 * k + 128], o_t[:, 128 * k : 128 * k + 128], ident32[:])
-                nc.scalar.copy(out=o_t[:, 512:1024], in_=o_b[:])
+                if q == 14:
+                    nc.scalar.copy(out=o_t[:, 0:512], in_=o_ps[:])
+                    o_b = ps_t.tile([P, 512], F32, name="o_b", tag="wt")
+                    for k in range(4):
+                        nc.tensor.transpose(o_b[:, 128 * k : 128 * k + 128], o_t[:, 128 * k : 128 * k + 128], ident32[:])
+                    nc.scalar.copy(out=o_t[:, 512:1024], in_=o_b[:])
 
         def leaf_tc(piece):
             lg = lgp.tile([P, 2048], BF16, name="lg%d" % piece, tag="lg", align_bytes=64)
@@ -334,7 +363,8 @@ def tile_softtreeensemble_pa_kernel(tc, x, W, b, leaf_w, out):
                 out=xraw[:, 2048 * kk : 2048 * kk + 2048].rearrange("p (k d) -> p k d", k=2),
                 in_=xv[:, 2 * kk : 2 * kk + 2, :],
             )
-        nc.scalar.dma_start(out=brows[0:NI, :], in_=b)
+            if kk == 0:
+                nc.sync.dma_start(out=brows[0:NI, :], in_=b)
         load_w(0)
         load_w(1)
         load_w(2)
@@ -348,60 +378,96 @@ def tile_softtreeensemble_pa_kernel(tc, x, W, b, leaf_w, out):
                     for u2 in range(2):
                         src = 512 * (2 * kk + k2) + 256 * g + 128 * u2
                         nc.tensor.transpose(bank[:, (2 * k2 + u2) * 128 : (2 * k2 + u2) * 128 + 128], xw[:, src : src + 128], ident32[:])
-                if g == 1:
-                    warm_pe(1)
                 dst = xg[:, 1024 * g + 512 * kk : 1024 * g + 512 * kk + 512].rearrange("p (k i u) -> p k i u", k=2, u=2)
                 srcv = bank[:].rearrange("p (k u i) -> p k i u", k=2, u=2)
                 if g == 0:
                     nc.vector.tensor_copy(out=dst, in_=srcv)
                 else:
                     nc.scalar.copy(out=dst, in_=srcv)
-        nc.vector.quantize_mx(out=xc[:].bitcast(FP8X4), scales=xs[:], in_=xg[:].bitcast(BF16))
+        for g in range(2):
+            nc.vector.quantize_mx(out=xc[:, 512 * g : 512 * g + 512].bitcast(FP8X4), scales=xs[:, 512 * g : 512 * g + 512], in_=xg[:, 1024 * g : 1024 * g + 1024].bitcast(BF16))
+
+        tr_w(0, 0)
+        cp_w(0, 0)
+        quant_w(0, nodes=(0, 1))
         bt = ps_t.tile([P, 1024], BF16, name="bt", tag="wt")
         nc.tensor.transpose(bt[:, 0:128], brows[:], ident16[:])
         nc.vector.tensor_copy(out=bias[:], in_=bt[:, 0:128])
-        nc.vector.tensor_scalar(out=nbias[:], in0=bias[:], scalar1=-1.0, scalar2=0.0, op0=ALU.mult, op1=ALU.add)
-
-        transpose_copy_w(0, 0)
-        transpose_copy_w(0, 1)
-        quant_w(0, 0)
-        quant_w(0, 1)
-        gates(0, 0)
-        transpose_copy_w(1, 0)
-        transpose_copy_w(1, 1)
-        load_w(3)
-        gates(0, 1)
-        transpose_copy_w(2, 0)
-        transpose_copy_w(2, 1)
+        tr_w(0, 1)
+        tr_w(0, 2)
+        cp_w(0, 1)
+        cp_w(0, 2)
+        mx_z(0, 0)
+        tr_w(1, 0)
+        tr_w(1, 1)
+        quant_w(0, nodes=(1, 2))
+        sig(0, 0)
+        cp_w(1, 0)
+        cp_w(1, 1)
+        mx_z(0, 1)
+        mx_z(0, 2)
+        tr_w(1, 2)
+        tr_w(1, 3)
+        sig(0, 1)
+        sig(0, 2)
         quant_w(1, 0)
-        quant_w(1, 1)
-        load_w(4)
-        gates(1, 0)
-        transpose_copy_w(3, 0)
-        gates(1, 1)
-        transpose_copy_w(3, 1)
+        load_w(3)
+        cp_w(1, 2)
+        cp_w(1, 3)
+        mx_z(1, 0)
+        mx_z(1, 1)
         tree_a(0)
-        quant_w(2)
+        quant_w(1, 1)
         tree_b(0)
+        load_w(4)
+        tr_w(2, 0)
+        tr_w(2, 1)
+        sig(1, 0)
+        sig(1, 1)
+        cp_w(2, 0)
+        cp_w(2, 1)
+        mx_z(1, 2)
+        mx_z(1, 3)
+        sig(1, 2)
+        sig(1, 3)
+        tr_w(2, 2)
+        tr_w(2, 3)
+        cp_w(2, 2)
+        cp_w(2, 3)
         load_w(5)
-        gates(2, 0)
-        transpose_copy_w(4, 0)
-        gates(2, 1)
-        transpose_copy_w(4, 1)
         tree_a(1, 0)
-        tree_a(1, 1)
-        quant_w(3)
+        quant_w(2, 0)
         tree_b(1, 0)
+        tr_w(3, 0)
+        tr_w(3, 1)
+        gates(2, 0)
+        quant_w(2, 1)
+        tree_a(1, 1)
         tree_b(1, 1)
+        cp_w(3, 0)
+        cp_w(3, 1)
+        tr_w(3, 2)
+        tr_w(3, 3)
+        gates(2, 1)
+        tree_a(2, 0)
+        quant_w(3, 0)
+        tree_b(2, 0)
+        cp_w(3, 2)
+        cp_w(3, 3)
+        transpose_copy_w(4, 0)
+        tree_a(2, 1)
+        quant_w(3, 1)
+        tree_b(2, 1)
+        transpose_copy_w(4, 1)
 
-        for it in range(3, nu + 2):
+        for it in range(3, nu + SL):
             if it in LEAF_LOAD_AT:
                 load_leaf(LEAF_LOAD_AT.index(it))
             load_w(it + 3)
             for half in range(2):
                 gates(it, half)
                 if half == 0:
-                    second(it - 2)
+                    second(it - SL)
                 else:
                     one_minus(it)
                 transpose_copy_w(it + 2, half)
@@ -410,15 +476,16 @@ def tile_softtreeensemble_pa_kernel(tc, x, W, b, leaf_w, out):
             leaf_unit = it - 1 < nu and units[it - 1]["kind"] == "leaf"
             if leaf_unit:
                 quant_w(it + 1)
-            tree_a(it - 1)
+            if it > 3:
+                tree_a(it - 1)
             if not leaf_unit:
                 quant_w(it + 1)
             if it - 1 in LEAF_WORK_AT:
                 leaf_q(LEAF_WORK_AT.index(it - 1))
-            tree_b(it - 1)
+            if it > 3:
+                tree_b(it - 1)
 
-        nc.vector.tensor_tensor(out=o_t[:, 1024:1536], in0=o_t[:, 512:1024], in1=last[0][:], op=ALU.add)
-        nc.vector.tensor_tensor(out=o_t[:, 1536:2048], in0=o_t[:, 1024:1536], in1=last[1][:], op=ALU.add)
+        nc.vector.tensor_tensor(out=o_t[:, 1536:2048], in0=o_t[:, 512:1024], in1=last[0][:], op=ALU.add)
         nc.sync.dma_start(
             out=out.rearrange("(p k) c -> p k c", k=4),
             in_=o_t[:, 1536:2048].rearrange("p (k c) -> p k c", k=4),

@@ -17,11 +17,19 @@ NI, NL = 63, 64
 FLOPS = 2 * B * D * NI * T + 2 * B * NL * T * LD
 
 PINNED = True
+SECOND_AT = 1
+QF = 1
 COPY_ON_V = {(1,1),(1,3)}
 SL = 3
-HV = {5, 8}
+HV = {5}
 H_ON_VECTOR = 0
-WARM_FIRST = 5
+WARM_FIRST = 6
+WX = 1
+WW = 1
+WT = 1
+WE = 2
+DZ = {0, 2}
+DZ0 = 3
 LEAF_LOAD_AT = [3, 5, 8, 11]
 LEAF_WORK_AT = [4, 7, 10, 13]
 
@@ -69,6 +77,12 @@ def tile_softtreeensemble_pa_kernel(tc, x, W, b, leaf_w, out):
         def warm_pe(n):
             for r in range(n):
                 nc.tensor.matmul(out=o_ps[:], lhsT=dz[:, 0:128], rhs=dz[:], start=True, stop=True)
+
+        def dummy(n):
+            if n:
+                d = ps_t.tile([P, 512], F32, name="dd", tag="wt")
+                for r in range(n):
+                    nc.tensor.matmul(out=d[:], lhsT=dz[:, 0:128], rhs=dz[:], start=True, stop=True)
 
         warm_pe(WARM_FIRST)
         ident32 = const.tile([P, P], F32, name="ident32")
@@ -193,6 +207,8 @@ def tile_softtreeensemble_pa_kernel(tc, x, W, b, leaf_w, out):
             c, s = wcs[u]
             if True:
                 z = ps_z.tile([P, 512], F32, name="z%d_%d" % (u, e), tag="z")
+                if e in DZ and u >= DZ0:
+                    nc.tensor.matmul(out=z[:], lhsT=dz[:, 0:128], rhs=dz[:], start=True, stop=True)
                 for g in range(2):
                     cols = slice(256 * e + 128 * g, 256 * e + 128 * g + 128)
                     nc.tensor.matmul_mx(
@@ -326,6 +342,7 @@ def tile_softtreeensemble_pa_kernel(tc, x, W, b, leaf_w, out):
                 )
                 if q == 14:
                     nc.scalar.copy(out=o_t[:, 0:512], in_=o_ps[:])
+                    dummy(WE)
                     o_b = ps_t.tile([P, 512], F32, name="o_b", tag="wt")
                     for k in range(4):
                         nc.tensor.transpose(o_b[:, 128 * k : 128 * k + 128], o_t[:, 128 * k : 128 * k + 128], ident32[:])
@@ -378,6 +395,7 @@ def tile_softtreeensemble_pa_kernel(tc, x, W, b, leaf_w, out):
                     for u2 in range(2):
                         src = 512 * (2 * kk + k2) + 256 * g + 128 * u2
                         nc.tensor.transpose(bank[:, (2 * k2 + u2) * 128 : (2 * k2 + u2) * 128 + 128], xw[:, src : src + 128], ident32[:])
+                warm_pe(WX)
                 dst = xg[:, 1024 * g + 512 * kk : 1024 * g + 512 * kk + 512].rearrange("p (k i u) -> p k i u", k=2, u=2)
                 srcv = bank[:].rearrange("p (k u i) -> p k i u", k=2, u=2)
                 if g == 0:
@@ -388,18 +406,22 @@ def tile_softtreeensemble_pa_kernel(tc, x, W, b, leaf_w, out):
             nc.vector.quantize_mx(out=xc[:, 512 * g : 512 * g + 512].bitcast(FP8X4), scales=xs[:, 512 * g : 512 * g + 512], in_=xg[:, 1024 * g : 1024 * g + 1024].bitcast(BF16))
 
         tr_w(0, 0)
+        warm_pe(WW)
         cp_w(0, 0)
         quant_w(0, nodes=(0, 1))
         bt = ps_t.tile([P, 1024], BF16, name="bt", tag="wt")
         nc.tensor.transpose(bt[:, 0:128], brows[:], ident16[:])
         nc.vector.tensor_copy(out=bias[:], in_=bt[:, 0:128])
         tr_w(0, 1)
+        warm_pe(WW)
         tr_w(0, 2)
+        warm_pe(WW)
         cp_w(0, 1)
         cp_w(0, 2)
         mx_z(0, 0)
         tr_w(1, 0)
         tr_w(1, 1)
+        warm_pe(WW)
         quant_w(0, nodes=(1, 2))
         sig(0, 0)
         cp_w(1, 0)
@@ -464,21 +486,28 @@ def tile_softtreeensemble_pa_kernel(tc, x, W, b, leaf_w, out):
             if it in LEAF_LOAD_AT:
                 load_leaf(LEAF_LOAD_AT.index(it))
             load_w(it + 3)
-            for half in range(2):
-                gates(it, half)
-                if half == 0:
+            for e in range(4):
+                if it < nu:
+                    mx_z(it, e)
+                if e == SECOND_AT:
                     second(it - SL)
-                else:
-                    one_minus(it)
-                transpose_copy_w(it + 2, half)
+                if it + 2 < nu:
+                    tr_w(it + 2, e)
+                elif it < nu:
+                    dummy(WT)
+                if it < nu:
+                    sig(it, e)
+                if it + 2 < nu:
+                    cp_w(it + 2, e)
+            one_minus(it)
             if it in LEAF_WORK_AT:
                 leaf_tc(LEAF_WORK_AT.index(it))
             leaf_unit = it - 1 < nu and units[it - 1]["kind"] == "leaf"
-            if leaf_unit:
+            if (leaf_unit or QF) and it != 4:
                 quant_w(it + 1)
             if it > 3:
                 tree_a(it - 1)
-            if not leaf_unit:
+            if not (leaf_unit or QF) or it == 4:
                 quant_w(it + 1)
             if it - 1 in LEAF_WORK_AT:
                 leaf_q(LEAF_WORK_AT.index(it - 1))

@@ -18,16 +18,17 @@ FLOPS = 2 * B * D * NI * T + 2 * B * NL * T * LD
 
 PINNED = True
 SECOND_AT = 1
-QF = 1
-COPY_ON_V = {(1,1),(1,3)}
+QF = 0
+COPY_ON_V = {(1, 1)}
 SL = 3
-HV = {5}
+HV = set()
 H_ON_VECTOR = 0
 WARM_FIRST = 6
 WX = 1
 WW = 1
 WT = 1
 WE = 2
+MH = 0
 DZ = {0, 2}
 DZ0 = 3
 LEAF_LOAD_AT = [3, 5, 8, 11]
@@ -251,11 +252,14 @@ def tile_softtreeensemble_pa_kernel(tc, x, W, b, leaf_w, out):
         p6c = {}
 
         def quant_p6(u, bb):
-            if bb == 0:
+            if bb != 1:
                 c = p6q.tile([P, 1024], U32, name="p6c%d" % u, tag="p6c", align_bytes=64)
                 s = p6q.tile([P, 1024], U8, name="p6s%d" % u, tag="p6s", align_bytes=64)
                 p6c[u] = (c, s)
             c, s = p6c[u]
+            if bb is None:
+                nc.vector.quantize_mx(out=c[:].bitcast(FP8X4), scales=s[:], in_=p6[u][:])
+                return
             nc.vector.quantize_mx(
                 out=c[:, 512 * bb : 512 * bb + 512].bitcast(FP8X4),
                 scales=s[:, 512 * bb : 512 * bb + 512],
@@ -301,8 +305,9 @@ def tile_softtreeensemble_pa_kernel(tc, x, W, b, leaf_w, out):
             un = units[u]
             if un["kind"] == "leaf":
                 if u != nu - 1:
-                    quant_p6(u, 0)
-                quant_p6(u, 1)
+                    quant_p6(u, None)
+                else:
+                    quant_p6(u, 1)
                 return
             par, chv, gv = mid_views(u, half)
             nc.vector.tensor_tensor(out=chv[:, :, 1, :], in0=par, in1=chv[:, :, 0, :], op=ALU.subtract)
@@ -505,13 +510,22 @@ def tile_softtreeensemble_pa_kernel(tc, x, W, b, leaf_w, out):
             leaf_unit = it - 1 < nu and units[it - 1]["kind"] == "leaf"
             if (leaf_unit or QF) and it != 4:
                 quant_w(it + 1)
-            if it > 3:
+            halved = it > 3 and it - 1 < nu and units[it - 1]["kind"] == "mid" and (it == 4 or MH == 2) and MH > 0
+            if halved:
+                for hf in range(2):
+                    tree_a(it - 1, hf)
+                    if MH == 1:
+                        tree_b(it - 1, hf)
+            elif it > 3:
                 tree_a(it - 1)
             if not (leaf_unit or QF) or it == 4:
                 quant_w(it + 1)
             if it - 1 in LEAF_WORK_AT:
                 leaf_q(LEAF_WORK_AT.index(it - 1))
-            if it > 3:
+            if halved and MH == 2:
+                for hf in range(2):
+                    tree_b(it - 1, hf)
+            elif it > 3 and not halved:
                 tree_b(it - 1)
 
         nc.vector.tensor_tensor(out=o_t[:, 1536:2048], in0=o_t[:, 512:1024], in1=last[0][:], op=ALU.add)

@@ -24,12 +24,14 @@ SL = 3
 HV = set()
 H_ON_VECTOR = 0
 WARM_FIRST = 6
-WX = 1
-WW = 1
-WT = 1
-WE = 2
+WX = 0
+WW = 0
+WE = 0
 MH = 0
-DZ = {0, 2}
+RUN = 2
+TB = 4
+HEARLY = 0
+DZ = set()
 DZ0 = 3
 LEAF_LOAD_AT = [3, 5, 8, 11]
 LEAF_WORK_AT = [4, 7, 10, 13]
@@ -65,12 +67,15 @@ def tile_softtreeensemble_pa_kernel(tc, x, W, b, leaf_w, out):
         p4p = ctx.enter_context(tc.tile_pool(name="p4p", bufs=1))
         p6p = ctx.enter_context(tc.tile_pool(name="p6p", bufs=2))
         p6q = ctx.enter_context(tc.tile_pool(name="p6q", bufs=3))
-        ps_t = ctx.enter_context(tc.psum_pool(name="ps_t", bufs=4))
-        ps_z = ctx.enter_context(tc.psum_pool(name="ps_z", bufs=3))
+        ps_t = ctx.enter_context(tc.psum_pool(name="ps_t", bufs=TB))
+        ps_z = ctx.enter_context(tc.psum_pool(name="ps_z", bufs=7 - TB))
         ps_o = ctx.enter_context(tc.psum_pool(name="ps_o", bufs=1))
         if PINNED:
             ctx.enter_context(tc.manual_schedule())
 
+        brows = const.tile([P, P], BF16, name="brows")
+        nc.vector.memset(brows[:], 0.0)
+        nc.scalar.dma_start(out=brows[0:NI, :], in_=b)
         dz = const.tile([P, 512], BF16, name="dz")
         nc.vector.memset(dz[:], 0.0)
         o_ps = ps_o.tile([P, 512], F32, name="o_ps")
@@ -90,8 +95,6 @@ def tile_softtreeensemble_pa_kernel(tc, x, W, b, leaf_w, out):
         make_identity(nc, ident32[:])
         ident16 = const.tile([P, P], BF16, name="ident16")
         make_identity(nc, ident16[:])
-        brows = const.tile([P, P], BF16, name="brows")
-        nc.vector.memset(brows[:], 0.0)
         warm = const.tile([P, 8], F32, name="warm")
         nc.vector.memset(warm[:], 0.0)
         nc.scalar.activation(out=warm[:, 4:5], in_=warm[:, 0:1], func=ACT.Sigmoid)
@@ -385,8 +388,6 @@ def tile_softtreeensemble_pa_kernel(tc, x, W, b, leaf_w, out):
                 out=xraw[:, 2048 * kk : 2048 * kk + 2048].rearrange("p (k d) -> p k d", k=2),
                 in_=xv[:, 2 * kk : 2 * kk + 2, :],
             )
-            if kk == 0:
-                nc.sync.dma_start(out=brows[0:NI, :], in_=b)
         load_w(0)
         load_w(1)
         load_w(2)
@@ -491,20 +492,25 @@ def tile_softtreeensemble_pa_kernel(tc, x, W, b, leaf_w, out):
             if it in LEAF_LOAD_AT:
                 load_leaf(LEAF_LOAD_AT.index(it))
             load_w(it + 3)
-            for e in range(4):
+            for e0 in range(0, 4, RUN):
+                es = range(e0, e0 + RUN)
                 if it < nu:
-                    mx_z(it, e)
-                if e == SECOND_AT:
+                    for e in es:
+                        mx_z(it, e)
+                if SECOND_AT in es:
                     second(it - SL)
-                if it + 2 < nu:
-                    tr_w(it + 2, e)
-                elif it < nu:
-                    dummy(WT)
                 if it < nu:
-                    sig(it, e)
+                    for e in es:
+                        sig(it, e)
+                    if e0 + RUN == 4 and HEARLY:
+                        one_minus(it)
                 if it + 2 < nu:
-                    cp_w(it + 2, e)
-            one_minus(it)
+                    for e in es:
+                        tr_w(it + 2, e)
+                    for e in es:
+                        cp_w(it + 2, e)
+            if not HEARLY:
+                one_minus(it)
             if it in LEAF_WORK_AT:
                 leaf_tc(LEAF_WORK_AT.index(it))
             leaf_unit = it - 1 < nu and units[it - 1]["kind"] == "leaf"

@@ -234,11 +234,24 @@ def tile_softtreeensemble_pa_kernel(tc, x, W, b, leaf_w, out):
                 nc.vector.tensor_scalar(out=pt["p1"][:, 512:1024], in0=pt["p1"][:, 0:512], scalar1=-1.0, scalar2=1.0, op0=ALU.mult, op1=ALU.add)
                 return
             if True:
-                nc.scalar.activation(out=gts[u][:, 512 * e : 512 * e + 512], in_=z[:], func=ACT.Sigmoid, bias=bias[:, n : n + 1], scale=1.0)
+                if units[u]["kind"] == "leaf":
+                    dst = gts[u][:].rearrange("p (c t i) -> p t c i", t=4, i=4)[:, e]
+                    src = z[:].rearrange("p (c i) -> p c i", i=4)
+                else:
+                    dst = gts[u][:, 512 * e : 512 * e + 512]
+                    src = z[:]
+                nc.scalar.activation(out=dst, in_=src, func=ACT.Sigmoid, bias=bias[:, n : n + 1], scale=1.0)
 
         def one_minus(u):
             if u < nu and units[u]["kind"] == "leaf" and u not in HV:
                 nc.scalar.activation(out=hts[u][:], in_=gts[u][:], func=ACT.Copy, bias=1.0, scale=-1.0)
+
+        def p5_views(u, hf):
+            lo = 512 * (units[u]["pj"] + 2 * hf)
+            par = pt["p4"][:, lo : lo + 1024].rearrange("p (j c i) -> p c j i", j=2, i=4)
+            gv = gts[u][:, 1024 * hf : 1024 * hf + 1024].rearrange("p (j c i) -> p c j i", j=2, i=4)
+            ch = pt["p5"][:, 2048 * hf : 2048 * hf + 2048].rearrange("p (c j b i) -> p b c j i", j=2, b=2, i=4)
+            return par, ch[:, 0], ch[:, 1], gv
 
         def mid_views(u, half):
             un = units[u]
@@ -274,23 +287,23 @@ def tile_softtreeensemble_pa_kernel(tc, x, W, b, leaf_w, out):
                 return
             un = units[u]
             if un["kind"] == "leaf":
-                par = pt["p5"][:, 512 * un["pj"] : 512 * un["pj"] + 2048].rearrange("p (t c i) -> p c t i", t=4, i=4)
+                par = pt["p5"][:, 512 * un["pj"] : 512 * un["pj"] + 2048].rearrange("p (m q i) -> p m i q", q=2, i=4)
                 if u in HV:
                     nc.vector.tensor_scalar(out=hts[u][:], in0=gts[u][:], scalar1=-1.0, scalar2=1.0, op0=ALU.mult, op1=ALU.add)
                 pg = p6p.tile([P, 4096], BF16, name="p6g%d" % u, tag="p6g", align_bytes=64)
                 p6[u] = pg
                 nc.vector.tensor_tensor(
-                    out=pg[:, 0:2048].rearrange("p (c i t) -> p c t i", i=4, t=4),
+                    out=pg[:, 0:2048].rearrange("p (i m q) -> p m i q", i=4, q=2),
                     in0=par,
-                    in1=gts[u][:].rearrange("p (t c i) -> p c t i", t=4, i=4),
+                    in1=gts[u][:].rearrange("p (m q i) -> p m i q", q=2, i=4),
                     op=ALU.mult,
                 )
                 if u == nu - 1:
                     quant_p6(u, 0)
                 nc.vector.tensor_tensor(
-                    out=pg[:, 2048:4096].rearrange("p (c i t) -> p c t i", i=4, t=4),
+                    out=pg[:, 2048:4096].rearrange("p (i m q) -> p m i q", i=4, q=2),
                     in0=par,
-                    in1=hts[u][:].rearrange("p (t c i) -> p c t i", t=4, i=4),
+                    in1=hts[u][:].rearrange("p (m q i) -> p m i q", q=2, i=4),
                     op=ALU.mult,
                 )
                 return
@@ -299,6 +312,11 @@ def tile_softtreeensemble_pa_kernel(tc, x, W, b, leaf_w, out):
                     pt["p4"] = p4p.tile([P, 8192], F32, name="p4")
                 else:
                     pt[un["ch"]] = pp.tile([P, 4096], F32, name="%s_%d" % (un["ch"], u), tag="p8")
+            if un["ch"] == "p5":
+                for hf in range(2):
+                    par, lv, rv, gv = p5_views(u, hf)
+                    nc.vector.tensor_tensor(out=lv, in0=par, in1=gv, op=ALU.mult)
+                return
             par, chv, gv = mid_views(u, half)
             nc.vector.tensor_tensor(out=chv[:, :, 0, :], in0=par, in1=gv, op=ALU.mult)
 
@@ -311,6 +329,11 @@ def tile_softtreeensemble_pa_kernel(tc, x, W, b, leaf_w, out):
                     quant_p6(u, None)
                 else:
                     quant_p6(u, 1)
+                return
+            if un["ch"] == "p5":
+                for hf in range(2):
+                    par, lv, rv, gv = p5_views(u, hf)
+                    nc.vector.tensor_tensor(out=rv, in0=par, in1=lv, op=ALU.subtract)
                 return
             par, chv, gv = mid_views(u, half)
             nc.vector.tensor_tensor(out=chv[:, :, 1, :], in0=par, in1=chv[:, :, 0, :], op=ALU.subtract)
@@ -382,7 +405,7 @@ def tile_softtreeensemble_pa_kernel(tc, x, W, b, leaf_w, out):
             )
 
         xraw = rawp.tile([P, 4096], BF16, name="xraw", tag="raw")
-        xv = x.rearrange("(p k) d -> p k d", k=4)
+        xv = x.rearrange("(k p) d -> p k d", k=4)
         for kk in range(2):
             nc.sync.dma_start(
                 out=xraw[:, 2048 * kk : 2048 * kk + 2048].rearrange("p (k d) -> p k d", k=2),

@@ -29,6 +29,13 @@ WW = 0
 WE = 0
 MH = 0
 RUN = 2
+ETAG = "wt"
+ET = {7, 10, 13}
+E0 = 0
+E1 = 1
+EC0 = 0
+EC1 = 1
+EL = 2
 TB = 4
 HEARLY = 0
 DZ = set()
@@ -69,6 +76,7 @@ def tile_softtreeensemble_pa_kernel(tc, x, W, b, leaf_w, out):
         p6q = ctx.enter_context(tc.tile_pool(name="p6q", bufs=3))
         ps_t = ctx.enter_context(tc.psum_pool(name="ps_t", bufs=TB))
         ps_z = ctx.enter_context(tc.psum_pool(name="ps_z", bufs=7 - TB))
+        ps_e = ps_t if ETAG == "wt" else ctx.enter_context(tc.psum_pool(name="ps_e", bufs=1))
         ps_o = ctx.enter_context(tc.psum_pool(name="ps_o", bufs=1))
         if PINNED:
             ctx.enter_context(tc.manual_schedule())
@@ -93,6 +101,9 @@ def tile_softtreeensemble_pa_kernel(tc, x, W, b, leaf_w, out):
         warm_pe(WARM_FIRST)
         ident32 = const.tile([P, P], F32, name="ident32")
         make_identity(nc, ident32[:])
+        nident32 = const.tile([P, P], F32, name="nident32")
+        nc.vector.tensor_scalar(out=nident32[:], in0=ident32[:], scalar1=-1.0, scalar2=0.0, op0=ALU.mult, op1=ALU.add)
+        pt5 = {}
         ident16 = const.tile([P, P], BF16, name="ident16")
         make_identity(nc, ident16[:])
         warm = const.tile([P, 8], F32, name="warm")
@@ -253,6 +264,24 @@ def tile_softtreeensemble_pa_kernel(tc, x, W, b, leaf_w, out):
             ch = pt["p5"][:, 2048 * hf : 2048 * hf + 2048].rearrange("p (c j b i) -> p b c j i", j=2, b=2, i=4)
             return par, ch[:, 0], ch[:, 1], gv
 
+        diff = {}
+
+        def tensor_rights(u, j):
+            if u not in ET:
+                return
+            lo = 512 * (units[u]["pj"] + 2 + j)
+            left = pt5[u][:, 2048:4096].rearrange("p (c t i) -> p t c i", t=4, i=4)[:, 2 * j]
+            d = ps_e.tile([P, 512], F32, name="d%d_%d" % (u, j), tag=ETAG)
+            diff[u, j] = d
+            nc.tensor.matmul(out=d[:], lhsT=ident32[:], rhs=pt["p4"][:, lo : lo + 512], start=True, stop=False)
+            nc.tensor.matmul(out=d[:].rearrange("p (c i) -> p c i", i=4), lhsT=nident32[:], rhs=left, start=False, stop=True)
+
+        def rights_out(u, j):
+            if u not in ET:
+                return
+            right = pt5[u][:, 2048:4096].rearrange("p (c t i) -> p t c i", t=4, i=4)[:, 2 * j + 1]
+            nc.scalar.copy(out=right, in_=diff[u, j][:].rearrange("p (c i) -> p c i", i=4))
+
         def mid_views(u, half):
             un = units[u]
             nn = 2 if un["kind"] == "top" else 4
@@ -312,6 +341,7 @@ def tile_softtreeensemble_pa_kernel(tc, x, W, b, leaf_w, out):
                     pt["p4"] = p4p.tile([P, 8192], F32, name="p4")
                 else:
                     pt[un["ch"]] = pp.tile([P, 4096], F32, name="%s_%d" % (un["ch"], u), tag="p8")
+                    pt5[u] = pt[un["ch"]]
             if un["ch"] == "p5":
                 for hf in range(2):
                     par, lv, rv, gv = p5_views(u, hf)
@@ -331,7 +361,7 @@ def tile_softtreeensemble_pa_kernel(tc, x, W, b, leaf_w, out):
                     quant_p6(u, 1)
                 return
             if un["ch"] == "p5":
-                for hf in range(2):
+                for hf in range(1 if u in ET else 2):
                     par, lv, rv, gv = p5_views(u, hf)
                     nc.vector.tensor_tensor(out=rv, in0=par, in1=lv, op=ALU.subtract)
                 return
@@ -517,6 +547,13 @@ def tile_softtreeensemble_pa_kernel(tc, x, W, b, leaf_w, out):
             load_w(it + 3)
             for e0 in range(0, 4, RUN):
                 es = range(e0, e0 + RUN)
+                hx = e0 // RUN
+                for j, at in ((0, E0), (1, E1)):
+                    if at == hx:
+                        tensor_rights(it - EL, j)
+                for j, at in ((0, EC0), (1, EC1)):
+                    if at == hx:
+                        rights_out(it - EL, j)
                 if it < nu:
                     for e in es:
                         mx_z(it, e)

@@ -21,11 +21,9 @@ SECOND_AT = 1
 QF = 0
 COPY_ON_V = {(1, 1)}
 SL = 3
-HV = set()
-H_ON_VECTOR = 0
 WARM_FIRST = 6
-WX = 0
-WW = 0
+WX = 1
+WW = 1
 WE = 0
 MH = 0
 RUN = 2
@@ -37,7 +35,8 @@ EC0 = 0
 EC1 = 1
 EL = 2
 TB = 4
-HEARLY = 0
+GB = 3
+HS = {8, 11, 14}
 DZ = set()
 DZ0 = 3
 LEAF_LOAD_AT = [3, 5, 8, 11]
@@ -68,8 +67,8 @@ def tile_softtreeensemble_pa_kernel(tc, x, W, b, leaf_w, out):
         grpp = ctx.enter_context(tc.tile_pool(name="grpp", bufs=3))
         lgp = ctx.enter_context(tc.tile_pool(name="lgp", bufs=2))
         wcp = ctx.enter_context(tc.tile_pool(name="wcp", bufs=2))
-        gp = ctx.enter_context(tc.tile_pool(name="gp", bufs=3))
-        hp = ctx.enter_context(tc.tile_pool(name="hp", bufs=2))
+        hp = ctx.enter_context(tc.tile_pool(name="hp", bufs=1))
+        gp = ctx.enter_context(tc.tile_pool(name="gp", bufs=GB))
         pp = ctx.enter_context(tc.tile_pool(name="pp", bufs=2))
         p4p = ctx.enter_context(tc.tile_pool(name="p4p", bufs=1))
         p6p = ctx.enter_context(tc.tile_pool(name="p6p", bufs=2))
@@ -118,9 +117,9 @@ def tile_softtreeensemble_pa_kernel(tc, x, W, b, leaf_w, out):
 
         raw = {}
         wg = {}
+        hts = {}
         wcs = {}
         gts = {}
-        hts = {}
         pt = {}
         p6 = {}
         lraw = {}
@@ -215,8 +214,6 @@ def tile_softtreeensemble_pa_kernel(tc, x, W, b, leaf_w, out):
             un = units[u]
             if u not in gts:
                 gts[u] = gp.tile([P, 2048], F32, name="g%d" % u, tag="g")
-                if un["kind"] == "leaf":
-                    hts[u] = hp.tile([P, 2048], F32, name="h%d" % u, tag="h")
                 if un["kind"] == "top":
                     pt["p1"] = pp.tile([P, 4096], F32, name="p1", tag="p8")
             c, s = wcs[u]
@@ -248,20 +245,19 @@ def tile_softtreeensemble_pa_kernel(tc, x, W, b, leaf_w, out):
                 if units[u]["kind"] == "leaf":
                     dst = gts[u][:].rearrange("p (c t i) -> p t c i", t=4, i=4)[:, e]
                     src = z[:].rearrange("p (c i) -> p c i", i=4)
+                elif units[u]["ch"] == "p5":
+                    dst = gts[u][:, 1024 * (e // 2) : 1024 * (e // 2) + 1024].rearrange("p (c j i) -> p j c i", j=2, i=4)[:, e % 2]
+                    src = z[:].rearrange("p (c i) -> p c i", i=4)
                 else:
                     dst = gts[u][:, 512 * e : 512 * e + 512]
                     src = z[:]
                 nc.scalar.activation(out=dst, in_=src, func=ACT.Sigmoid, bias=bias[:, n : n + 1], scale=1.0)
 
-        def one_minus(u):
-            if u < nu and units[u]["kind"] == "leaf" and u not in HV:
-                nc.scalar.activation(out=hts[u][:], in_=gts[u][:], func=ACT.Copy, bias=1.0, scale=-1.0)
-
-        def p5_views(u, hf):
-            lo = 512 * (units[u]["pj"] + 2 * hf)
-            par = pt["p4"][:, lo : lo + 1024].rearrange("p (j c i) -> p c j i", j=2, i=4)
-            gv = gts[u][:, 1024 * hf : 1024 * hf + 1024].rearrange("p (j c i) -> p c j i", j=2, i=4)
-            ch = pt["p5"][:, 2048 * hf : 2048 * hf + 2048].rearrange("p (c j b i) -> p b c j i", j=2, b=2, i=4)
+        def p5_views(u, n):
+            lo = 512 * units[u]["pj"]
+            par = pt["p4"][:, lo : lo + 1024 * n].rearrange("p (h m i) -> p h m i", h=n, i=4)
+            gv = gts[u][:, 0 : 1024 * n].rearrange("p (h m i) -> p h m i", h=n, i=4)
+            ch = pt["p5"][:, 0 : 2048 * n].rearrange("p (h m b i) -> p b h m i", h=n, b=2, i=4)
             return par, ch[:, 0], ch[:, 1], gv
 
         diff = {}
@@ -269,12 +265,14 @@ def tile_softtreeensemble_pa_kernel(tc, x, W, b, leaf_w, out):
         def tensor_rights(u, j):
             if u not in ET:
                 return
-            lo = 512 * (units[u]["pj"] + 2 + j)
+            lo = 512 * (units[u]["pj"] + 2)
+            par = pt["p4"][:, lo : lo + 1024].rearrange("p (c j i) -> p j c i", j=2, i=4)[:, j]
             left = pt5[u][:, 2048:4096].rearrange("p (c t i) -> p t c i", t=4, i=4)[:, 2 * j]
             d = ps_e.tile([P, 512], F32, name="d%d_%d" % (u, j), tag=ETAG)
             diff[u, j] = d
-            nc.tensor.matmul(out=d[:], lhsT=ident32[:], rhs=pt["p4"][:, lo : lo + 512], start=True, stop=False)
-            nc.tensor.matmul(out=d[:].rearrange("p (c i) -> p c i", i=4), lhsT=nident32[:], rhs=left, start=False, stop=True)
+            dv = d[:].rearrange("p (c i) -> p c i", i=4)
+            nc.tensor.matmul(out=dv, lhsT=ident32[:], rhs=par, start=True, stop=False)
+            nc.tensor.matmul(out=dv, lhsT=nident32[:], rhs=left, start=False, stop=True)
 
         def rights_out(u, j):
             if u not in ET:
@@ -289,6 +287,11 @@ def tile_softtreeensemble_pa_kernel(tc, x, W, b, leaf_w, out):
             j0 = 0
             if half is not None:
                 nn, j0 = 2, 2 * half
+            if un["ch"] == "p4":
+                par = pt[un["par"]][:, 512 * (un["pj"] + j0) : 512 * (un["pj"] + j0 + nn)].rearrange("p (j c i) -> p j c i", j=nn, i=4)
+                chv = pt["p4"][:, 1024 * (un["cj"] + j0) : 1024 * (un["cj"] + j0 + nn)].rearrange("p (j c b i) -> p j b c i", j=nn, b=2, i=4)
+                gv = gts[u][:, 512 * j0 : 512 * (j0 + nn)].rearrange("p (j c i) -> p j c i", j=nn, i=4)
+                return par, chv, gv
             par = pt[un["par"]][:, 512 * (un["pj"] + j0) : 512 * (un["pj"] + j0 + nn)].rearrange("p (j w) -> p j w", w=512)
             chv = pt[un["ch"]][:, 1024 * (un["cj"] + j0) : 1024 * (un["cj"] + j0 + nn)].rearrange("p (j b w) -> p j b w", b=2, w=512)
             gv = gts[u][:, g0 + 512 * j0 : g0 + 512 * (j0 + nn)].rearrange("p (j w) -> p j w", w=512)
@@ -317,8 +320,6 @@ def tile_softtreeensemble_pa_kernel(tc, x, W, b, leaf_w, out):
             un = units[u]
             if un["kind"] == "leaf":
                 par = pt["p5"][:, 512 * un["pj"] : 512 * un["pj"] + 2048].rearrange("p (m q i) -> p m i q", q=2, i=4)
-                if u in HV:
-                    nc.vector.tensor_scalar(out=hts[u][:], in0=gts[u][:], scalar1=-1.0, scalar2=1.0, op0=ALU.mult, op1=ALU.add)
                 pg = p6p.tile([P, 4096], BF16, name="p6g%d" % u, tag="p6g", align_bytes=64)
                 p6[u] = pg
                 nc.vector.tensor_tensor(
@@ -329,11 +330,21 @@ def tile_softtreeensemble_pa_kernel(tc, x, W, b, leaf_w, out):
                 )
                 if u == nu - 1:
                     quant_p6(u, 0)
-                nc.vector.tensor_tensor(
-                    out=pg[:, 2048:4096].rearrange("p (i m q) -> p m i q", i=4, q=2),
-                    in0=par,
-                    in1=hts[u][:].rearrange("p (m q i) -> p m i q", q=2, i=4),
-                    op=ALU.mult,
+                if u in HS:
+                    nc.vector.tensor_tensor(
+                        out=pg[:, 2048:4096].rearrange("p (i m q) -> p m i q", i=4, q=2),
+                        in0=par,
+                        in1=hts[u][:].rearrange("p (m q i) -> p m i q", q=2, i=4),
+                        op=ALU.mult,
+                    )
+                    return
+                nc.vector.scalar_tensor_tensor(
+                    out=pg[:, 2048:4096].rearrange("p (i m) -> p m i", i=4),
+                    in0=gts[u][:].rearrange("p (m i) -> p m i", i=4),
+                    scalar=1.0,
+                    in1=pt["p5"][:, 512 * un["pj"] : 512 * un["pj"] + 2048].rearrange("p (m i) -> p m i", i=4),
+                    op0=ALU.subtract,
+                    op1=ALU.mult,
                 )
                 return
             if un["cj"] == 0 and not half:
@@ -343,12 +354,11 @@ def tile_softtreeensemble_pa_kernel(tc, x, W, b, leaf_w, out):
                     pt[un["ch"]] = pp.tile([P, 4096], F32, name="%s_%d" % (un["ch"], u), tag="p8")
                     pt5[u] = pt[un["ch"]]
             if un["ch"] == "p5":
-                for hf in range(2):
-                    par, lv, rv, gv = p5_views(u, hf)
-                    nc.vector.tensor_tensor(out=lv, in0=par, in1=gv, op=ALU.mult)
+                par, lv, rv, gv = p5_views(u, 2)
+                nc.vector.tensor_tensor(out=lv, in0=par, in1=gv, op=ALU.mult)
                 return
             par, chv, gv = mid_views(u, half)
-            nc.vector.tensor_tensor(out=chv[:, :, 0, :], in0=par, in1=gv, op=ALU.mult)
+            nc.vector.tensor_tensor(out=chv[:, :, 0], in0=par, in1=gv, op=ALU.mult)
 
         def tree_b(u, half=None):
             if u < 0 or u >= nu:
@@ -361,12 +371,11 @@ def tile_softtreeensemble_pa_kernel(tc, x, W, b, leaf_w, out):
                     quant_p6(u, 1)
                 return
             if un["ch"] == "p5":
-                for hf in range(1 if u in ET else 2):
-                    par, lv, rv, gv = p5_views(u, hf)
-                    nc.vector.tensor_tensor(out=rv, in0=par, in1=lv, op=ALU.subtract)
+                par, lv, rv, gv = p5_views(u, 1 if u in ET else 2)
+                nc.vector.tensor_tensor(out=rv, in0=par, in1=lv, op=ALU.subtract)
                 return
             par, chv, gv = mid_views(u, half)
-            nc.vector.tensor_tensor(out=chv[:, :, 1, :], in0=par, in1=chv[:, :, 0, :], op=ALU.subtract)
+            nc.vector.tensor_tensor(out=chv[:, :, 1], in0=par, in1=chv[:, :, 0], op=ALU.subtract)
 
         o_t = const.tile([P, 2048], F32, name="o_t")
         last = {}
@@ -423,8 +432,14 @@ def tile_softtreeensemble_pa_kernel(tc, x, W, b, leaf_w, out):
                 banks.append(bank)
             for k in range(2):
                 nc.scalar.copy(
-                    out=lg[:, 1024 * k : 1024 * k + 1024].rearrange("p (b c t) -> p b c t", b=2, t=4),
-                    in_=banks[k][:].rearrange("p (b t c) -> p b c t", b=2, t=4),
+                    out=lg[:, 1024 * k : 1024 * k + 512].rearrange("p (c t) -> p c t", t=4),
+                    in_=banks[k][:, 0:512].rearrange("p (t c) -> p c t", t=4),
+                )
+                nc.scalar.activation(
+                    out=lg[:, 1024 * k + 512 : 1024 * k + 1024].rearrange("p (c t) -> p c t", t=4),
+                    in_=banks[k][:, 512:1024].rearrange("p (t c) -> p c t", t=4),
+                    func=ACT.Copy,
+                    scale=-1.0,
                 )
 
         def leaf_q(piece):
@@ -562,15 +577,14 @@ def tile_softtreeensemble_pa_kernel(tc, x, W, b, leaf_w, out):
                 if it < nu:
                     for e in es:
                         sig(it, e)
-                    if e0 + RUN == 4 and HEARLY:
-                        one_minus(it)
                 if it + 2 < nu:
                     for e in es:
                         tr_w(it + 2, e)
                     for e in es:
                         cp_w(it + 2, e)
-            if not HEARLY:
-                one_minus(it)
+            if it in HS:
+                hts[it] = hp.tile([P, 2048], F32, name="h%d" % it, tag="h")
+                nc.scalar.activation(out=hts[it][:], in_=gts[it][:], func=ACT.Copy, bias=-1.0, scale=1.0)
             if it in LEAF_WORK_AT:
                 leaf_tc(LEAF_WORK_AT.index(it))
             leaf_unit = it - 1 < nu and units[it - 1]["kind"] == "leaf"

@@ -19,14 +19,17 @@ FLOPS = 2 * B * D * NI * T + 2 * B * NL * T * LD
 PINNED = True
 SECOND_AT = 1
 QF = 0
-COPY_ON_V = {(1, 1)}
+COPY_ON_V = {(5, 1)}
 SL = 3
 WARM_FIRST = 6
 WX = 1
 WW = 1
-WE = 0
+WE = 2
 MH = 0
 RUN = 2
+RAMP = 0
+SPLIT = 1
+SPLIT2 = 1
 ETAG = "wt"
 ET = {7, 10, 13}
 E0 = 0
@@ -40,7 +43,7 @@ HS = {8, 11, 14}
 DZ = set()
 DZ0 = 3
 LEAF_LOAD_AT = [3, 5, 8, 11]
-LEAF_WORK_AT = [4, 7, 10, 13]
+LEAF_WORK_AT = [5, 8, 11, 14]
 
 
 def build_units():
@@ -338,14 +341,15 @@ def tile_softtreeensemble_pa_kernel(tc, x, W, b, leaf_w, out):
                         op=ALU.mult,
                     )
                     return
-                nc.vector.scalar_tensor_tensor(
-                    out=pg[:, 2048:4096].rearrange("p (i m) -> p m i", i=4),
-                    in0=gts[u][:].rearrange("p (m i) -> p m i", i=4),
+                for i0, ni in [(0, 2), (2, 2)] if u == nu - 1 and SPLIT else [(0, 4)]:
+                  nc.vector.scalar_tensor_tensor(
+                    out=pg[:, 2048:4096].rearrange("p (i m) -> p m i", i=4)[:, :, i0 : i0 + ni],
+                    in0=gts[u][:].rearrange("p (m i) -> p m i", i=4)[:, :, i0 : i0 + ni],
                     scalar=1.0,
-                    in1=pt["p5"][:, 512 * un["pj"] : 512 * un["pj"] + 2048].rearrange("p (m i) -> p m i", i=4),
+                    in1=pt["p5"][:, 512 * un["pj"] : 512 * un["pj"] + 2048].rearrange("p (m i) -> p m i", i=4)[:, :, i0 : i0 + ni],
                     op0=ALU.subtract,
                     op1=ALU.mult,
-                )
+                  )
                 return
             if un["cj"] == 0 and not half:
                 if un["ch"] == "p4":
@@ -368,7 +372,13 @@ def tile_softtreeensemble_pa_kernel(tc, x, W, b, leaf_w, out):
                 if u != nu - 1:
                     quant_p6(u, None)
                 else:
-                    quant_p6(u, 1)
+                    for c0, w in [(0, 256), (256, 256)] if SPLIT else [(0, 512)]:
+                        c, s = p6c[u]
+                        nc.vector.quantize_mx(
+                            out=c[:, 512 + c0 : 512 + c0 + w].bitcast(FP8X4),
+                            scales=s[:, 512 + c0 : 512 + c0 + w],
+                            in_=p6[u][:, 2048 + 4 * c0 : 2048 + 4 * (c0 + w)],
+                        )
                 return
             if un["ch"] == "p5":
                 par, lv, rv, gv = p5_views(u, 1 if u in ET else 2)
@@ -387,9 +397,10 @@ def tile_softtreeensemble_pa_kernel(tc, x, W, b, leaf_w, out):
             for bb in range(2):
                 q = units[u]["q0"] + bb
                 if q == 15:
-                    o2 = ps_t.tile([P, 512], F32, name="o2", tag="wt")
-                    last[0] = o2
                     for k in range(4):
+                        if k == 0 or (k == 2 and SPLIT2):
+                            o2 = ps_t.tile([P, 512], F32, name="o2_%d" % k, tag="wt")
+                            last[k // 2] = o2
                         cols = slice(512 * bb + 128 * k, 512 * bb + 128 * k + 128)
                         nc.tensor.matmul_mx(
                             out=o2[:, 128 * k : 128 * k + 128],
@@ -554,7 +565,8 @@ def tile_softtreeensemble_pa_kernel(tc, x, W, b, leaf_w, out):
         tree_a(2, 1)
         quant_w(3, 1)
         tree_b(2, 1)
-        transpose_copy_w(4, 1)
+        if not RAMP:
+            transpose_copy_w(4, 1)
 
         for it in range(3, nu + SL):
             if it in LEAF_LOAD_AT:
@@ -577,11 +589,13 @@ def tile_softtreeensemble_pa_kernel(tc, x, W, b, leaf_w, out):
                 if it < nu:
                     for e in es:
                         sig(it, e)
-                if it + 2 < nu:
-                    for e in es:
-                        tr_w(it + 2, e)
-                    for e in es:
-                        cp_w(it + 2, e)
+                ahead = [(it + 2, e) for e in es] if it + 2 < nu else []
+                if it == 3 and RAMP:
+                    ahead = [(4, 2), (4, 3)] if e0 == 0 else [(5, e) for e in range(4)]
+                for u, e in ahead:
+                    tr_w(u, e)
+                for u, e in ahead:
+                    cp_w(u, e)
             if it in HS:
                 hts[it] = hp.tile([P, 2048], F32, name="h%d" % it, tag="h")
                 nc.scalar.activation(out=hts[it][:], in_=gts[it][:], func=ACT.Copy, bias=-1.0, scale=1.0)
@@ -608,7 +622,10 @@ def tile_softtreeensemble_pa_kernel(tc, x, W, b, leaf_w, out):
             elif it > 3 and not halved:
                 tree_b(it - 1)
 
-        nc.vector.tensor_tensor(out=o_t[:, 1536:2048], in0=o_t[:, 512:1024], in1=last[0][:], op=ALU.add)
+        for c0, w in [(0, 256), (256, 256)] if SPLIT else [(0, 512)]:
+            nc.vector.tensor_tensor(
+                out=o_t[:, 1536 + c0 : 1536 + c0 + w], in0=o_t[:, 512 + c0 : 512 + c0 + w], in1=(last[0] if c0 == 0 or not SPLIT2 else last[1])[:, c0 : c0 + w], op=ALU.add
+            )
         nc.sync.dma_start(
             out=out.rearrange("(p k) c -> p k c", k=4),
             in_=o_t[:, 1536:2048].rearrange("p (k c) -> p k c", k=4),

from contextlib import ExitStack

import concourse.mybir as mybir
from concourse.masks import make_identity

F32 = mybir.dt.float32
BF16 = mybir.dt.bfloat16
U32 = mybir.dt.uint32
U8 = mybir.dt.uint8
FP8X4 = mybir.dt.float8_e4m3fn_x4
ALU = mybir.AluOpType
ACT = mybir.ActivationFunctionType

P = 128
B, D, T, LD = 512, 1024, 128, 128
NI, NL = 63, 64
FLOPS = 2 * B * D * NI * T + 2 * B * NL * T * LD

PINNED = True
SECOND_AT = 1
QF = 0
COPY_ON_V = {(5, 1)}
SL = 3
WARM_FIRST = 6
WX = 1
WW = 1
WE = 2
MH = 0
RUN = 2
RAMP = 0
SPLIT = 1
SPLIT2 = 1
ETAG = "wt"
ET = {7, 10, 13}
E0 = 0
E1 = 1
EC0 = 0
EC1 = 1
EL = 2
TB = 4
GB = 3
HS = {8, 11, 14}
DZ = set()
DZ0 = 3
LEAF_LOAD_AT = [3, 5, 8, 11]
LEAF_WORK_AT = [5, 8, 11, 14]


def build_units():
    units = [
        dict(n0=0, nn=3, kind="top", par="p1", pj=0, ch="p2", cj=0),
        dict(n0=3, nn=4, kind="mid", par="p2", pj=0, ch="p3", cj=0),
        dict(n0=7, nn=4, kind="mid", par="p3", pj=0, ch="p4", cj=0),
        dict(n0=11, nn=4, kind="mid", par="p3", pj=4, ch="p4", cj=4),
    ]
    for a in range(4):
        units.append(dict(n0=15 + 4 * a, nn=4, kind="mid", par="p4", pj=4 * a, ch="p5", cj=0))
        for hf in range(2):
            units.append(dict(n0=31 + 8 * a + 4 * hf, nn=4, kind="leaf", par="p5", pj=4 * hf, q0=2 * (2 * a + hf)))
    return units


def tile_softtreeensemble_pa_kernel(tc, x, W, b, leaf_w, out):
    nc = tc.nc
    units = build_units()
    nu = len(units)
    with ExitStack() as ctx:
        const = ctx.enter_context(tc.tile_pool(name="const", bufs=1))
        rawp = ctx.enter_context(tc.tile_pool(name="rawp", bufs=4))
        grpp = ctx.enter_context(tc.tile_pool(name="grpp", bufs=3))
        lgp = ctx.enter_context(tc.tile_pool(name="lgp", bufs=2))
        wcp = ctx.enter_context(tc.tile_pool(name="wcp", bufs=2))
        hp = ctx.enter_context(tc.tile_pool(name="hp", bufs=1))
        gp = ctx.enter_context(tc.tile_pool(name="gp", bufs=GB))
        pp = ctx.enter_context(tc.tile_pool(name="pp", bufs=2))
        p4p = ctx.enter_context(tc.tile_pool(name="p4p", bufs=1))
        p6p = ctx.enter_context(tc.tile_pool(name="p6p", bufs=2))
        p6q = ctx.enter_context(tc.tile_pool(name="p6q", bufs=3))
        ps_t = ctx.enter_context(tc.psum_pool(name="ps_t", bufs=TB))
        ps_z = ctx.enter_context(tc.psum_pool(name="ps_z", bufs=7 - TB))
        ps_e = ps_t if ETAG == "wt" else ctx.enter_context(tc.psum_pool(name="ps_e", bufs=1))
        ps_o = ctx.enter_context(tc.psum_pool(name="ps_o", bufs=1))
        if PINNED:
            ctx.enter_context(tc.manual_schedule())

        brows = const.tile([P, P], BF16, name="brows")
        nc.vector.memset(brows[:], 0.0)
        nc.scalar.dma_start(out=brows[0:NI, :], in_=b)
        dz = const.tile([P, 512], BF16, name="dz")
        nc.vector.memset(dz[:], 0.0)
        o_ps = ps_o.tile([P, 512], F32, name="o_ps")

        def warm_pe(n):
            for r in range(n):
                nc.tensor.matmul(out=o_ps[:], lhsT=dz[:, 0:128], rhs=dz[:], start=True, stop=True)

        def dummy(n):
            if n:
                d = ps_t.tile([P, 512], F32, name="dd", tag="wt")
                for r in range(n):
                    nc.tensor.matmul(out=d[:], lhsT=dz[:, 0:128], rhs=dz[:], start=True, stop=True)

        warm_pe(WARM_FIRST)
        ident32 = const.tile([P, P], F32, name="ident32")
        make_identity(nc, ident32[:])
        nident32 = const.tile([P, P], F32, name="nident32")
        nc.vector.tensor_scalar(out=nident32[:], in0=ident32[:], scalar1=-1.0, scalar2=0.0, op0=ALU.mult, op1=ALU.add)
        pt5 = {}
        ident16 = const.tile([P, P], BF16, name="ident16")
        make_identity(nc, ident16[:])
        warm = const.tile([P, 8], F32, name="warm")
        nc.vector.memset(warm[:], 0.0)
        nc.scalar.activation(out=warm[:, 4:5], in_=warm[:, 0:1], func=ACT.Sigmoid)
        bias = const.tile([P, P], F32, name="bias")
        nbias = const.tile([P, P], F32, name="nbias")
        xc = const.tile([P, 1024], U32, name="xc", align_bytes=64)
        xs = const.tile([P, 1024], U8, name="xs", align_bytes=64)
        lwc = const.tile([P, 2048], U32, name="lwc", align_bytes=64)
        lws = const.tile([P, 2048], U8, name="lws", align_bytes=64)

        raw = {}
        wg = {}
        hts = {}
        wcs = {}
        gts = {}
        pt = {}
        p6 = {}
        lraw = {}
        lgs = {}

        def load_w(u):
            if u >= nu:
                return
            n0, nn = units[u]["n0"], units[u]["nn"]
            r = rawp.tile([P, 4096], BF16, name="raw%d" % u, tag="raw")
            for e0, ne in ([(0, 1), (1, 2)] if u == 0 else [(0, 2), (2, 2)] if u == 1 else [(0, nn)]):
                nc.sync.dma_start(
                    out=r[:, e0 * 1024 : (e0 + ne) * 1024].rearrange("p (n d) -> p n d", n=ne),
                    in_=W[n0 + e0 : n0 + e0 + ne].rearrange("n t d -> t n d"),
                )
            raw[u] = r

        def load_leaf(piece):
            r = rawp.tile([P, 4096], BF16, name="lraw%d" % piece, tag="raw")
            nc.sync.dma_start(
                out=r[:, 0:2048].rearrange("p (j t) -> p j t", j=16),
                in_=leaf_w[16 * piece : 16 * piece + 16].rearrange("j c t -> c j t"),
            )
            lraw[piece] = r

        def halves(u):
            nn = units[u]["nn"]
            if nn == 3:
                return [[0], [1, 2]]
            return [[0, 1], [2, 3]]

        wts = {}

        def tr_w(u, e):
            rw = raw[u][:].bitcast(F32)
            wt = ps_t.tile([P, 512], F32, name="wt%d_%d" % (u, e), tag="wt")
            for s in range(4):
                nc.tensor.transpose(wt[:, 128 * s : 128 * s + 128], rw[:, 512 * e + 128 * s : 512 * e + 128 * s + 128], ident32[:])
            wts[u, e] = wt

        def cp_w(u, e):
            if u not in wg:
                wg[u] = grpp.tile([P, 2048], F32, name="wg%d" % u, tag="grp", align_bytes=64)
            copy = nc.vector.tensor_copy if (u, e) in COPY_ON_V else nc.scalar.copy
            copy(
                out=wg[u][:, 512 * e : 512 * e + 512].rearrange("p (g m u) -> p g m u", g=2, u=2),
                in_=wts[u, e][:].rearrange("p (g u m) -> p g m u", g=2, u=2),
            )

        def transpose_copy_w(u, half):
            if u >= nu:
                return
            for e in halves(u)[half]:
                tr_w(u, e)
            for e in halves(u)[half]:
                cp_w(u, e)

        def quant_w(u, half=None, nodes=None):
            if u >= nu:
                return
            if u not in wcs:
                wcs[u] = (
                    wcp.tile([P, 1024], U32, name="wc%d" % u, tag="wc", align_bytes=64),
                    wcp.tile([P, 1024], U8, name="ws%d" % u, tag="ws", align_bytes=64),
                )
            c, s = wcs[u]
            if nodes is not None:
                parts = [nodes]
            elif half is None:
                parts = [(0, 4)]
            else:
                es = halves(u)[half]
                parts = [(es[0], len(es))]
            for e0, ne in parts:
                nc.vector.quantize_mx(
                    out=c[:, 256 * e0 : 256 * (e0 + ne)].bitcast(FP8X4),
                    scales=s[:, 256 * e0 : 256 * (e0 + ne)],
                    in_=wg[u][:, 512 * e0 : 512 * (e0 + ne)].bitcast(BF16),
                )

        def gates(u, half):
            if u >= nu:
                return
            for e in halves(u)[half]:
                mx_z(u, e)
            for e in halves(u)[half]:
                sig(u, e)

        zts = {}

        def mx_z(u, e):
            un = units[u]
            if u not in gts:
                gts[u] = gp.tile([P, 2048], F32, name="g%d" % u, tag="g")
                if un["kind"] == "top":
                    pt["p1"] = pp.tile([P, 4096], F32, name="p1", tag="p8")
            c, s = wcs[u]
            if True:
                z = ps_z.tile([P, 512], F32, name="z%d_%d" % (u, e), tag="z")
                if e in DZ and u >= DZ0:
                    nc.tensor.matmul(out=z[:], lhsT=dz[:, 0:128], rhs=dz[:], start=True, stop=True)
                for g in range(2):
                    cols = slice(256 * e + 128 * g, 256 * e + 128 * g + 128)
                    nc.tensor.matmul_mx(
                        out=z[:],
                        lhsT=c[:, cols].bitcast(FP8X4),
                        lhsT_scale=s[:, cols],
                        rhs=xc[:, 512 * g : 512 * g + 512].bitcast(FP8X4),
                        rhs_scale=xs[:, 512 * g : 512 * g + 512],
                        start=(g == 0),
                        stop=(g == 1),
                    )
                zts[u, e] = z

        def sig(u, e):
            n = units[u]["n0"] + e
            z = zts[u, e]
            if n == 0:
                nc.scalar.activation(out=pt["p1"][:, 0:512], in_=z[:], func=ACT.Sigmoid, bias=bias[:, 0:1], scale=1.0)
                nc.vector.tensor_scalar(out=pt["p1"][:, 512:1024], in0=pt["p1"][:, 0:512], scalar1=-1.0, scalar2=1.0, op0=ALU.mult, op1=ALU.add)
                return
            if True:
                if units[u]["kind"] == "leaf":
                    dst = gts[u][:].rearrange("p (c t i) -> p t c i", t=4, i=4)[:, e]
                    src = z[:].rearrange("p (c i) -> p c i", i=4)
                elif units[u]["ch"] == "p5":
                    dst = gts[u][:, 1024 * (e // 2) : 1024 * (e // 2) + 1024].rearrange("p (c j i) -> p j c i", j=2, i=4)[:, e % 2]
                    src = z[:].rearrange("p (c i) -> p c i", i=4)
                else:
                    dst = gts[u][:, 512 * e : 512 * e + 512]
                    src = z[:]
                nc.scalar.activation(out=dst, in_=src, func=ACT.Sigmoid, bias=bias[:, n : n + 1], scale=1.0)

        def p5_views(u, n):
            lo = 512 * units[u]["pj"]
            par = pt["p4"][:, lo : lo + 1024 * n].rearrange("p (h m i) -> p h m i", h=n, i=4)
            gv = gts[u][:, 0 : 1024 * n].rearrange("p (h m i) -> p h m i", h=n, i=4)
            ch = pt["p5"][:, 0 : 2048 * n].rearrange("p (h m b i) -> p b h m i", h=n, b=2, i=4)
            return par, ch[:, 0], ch[:, 1], gv

        diff = {}

        def tensor_rights(u, j):
            if u not in ET:
                return
            lo = 512 * (units[u]["pj"] + 2)
            par = pt["p4"][:, lo : lo + 1024].rearrange("p (c j i) -> p j c i", j=2, i=4)[:, j]
            left = pt5[u][:, 2048:4096].rearrange("p (c t i) -> p t c i", t=4, i=4)[:, 2 * j]
            d = ps_e.tile([P, 512], F32, name="d%d_%d" % (u, j), tag=ETAG)
            diff[u, j] = d
            dv = d[:].rearrange("p (c i) -> p c i", i=4)
            nc.tensor.matmul(out=dv, lhsT=ident32[:], rhs=par, start=True, stop=False)
            nc.tensor.matmul(out=dv, lhsT=nident32[:], rhs=left, start=False, stop=True)

        def rights_out(u, j):
            if u not in ET:
                return
            right = pt5[u][:, 2048:4096].rearrange("p (c t i) -> p t c i", t=4, i=4)[:, 2 * j + 1]
            nc.scalar.copy(out=right, in_=diff[u, j][:].rearrange("p (c i) -> p c i", i=4))

        def mid_views(u, half):
            un = units[u]
            nn = 2 if un["kind"] == "top" else 4
            g0 = 512 if un["kind"] == "top" else 0
            j0 = 0
            if half is not None:
                nn, j0 = 2, 2 * half
            if un["ch"] == "p4":
                par = pt[un["par"]][:, 512 * (un["pj"] + j0) : 512 * (un["pj"] + j0 + nn)].rearrange("p (j c i) -> p j c i", j=nn, i=4)
                chv = pt["p4"][:, 1024 * (un["cj"] + j0) : 1024 * (un["cj"] + j0 + nn)].rearrange("p (j c b i) -> p j b c i", j=nn, b=2, i=4)
                gv = gts[u][:, 512 * j0 : 512 * (j0 + nn)].rearrange("p (j c i) -> p j c i", j=nn, i=4)
                return par, chv, gv
            par = pt[un["par"]][:, 512 * (un["pj"] + j0) : 512 * (un["pj"] + j0 + nn)].rearrange("p (j w) -> p j w", w=512)
            chv = pt[un["ch"]][:, 1024 * (un["cj"] + j0) : 1024 * (un["cj"] + j0 + nn)].rearrange("p (j b w) -> p j b w", b=2, w=512)
            gv = gts[u][:, g0 + 512 * j0 : g0 + 512 * (j0 + nn)].rearrange("p (j w) -> p j w", w=512)
            return par, chv, gv

        p6c = {}

        def quant_p6(u, bb):
            if bb != 1:
                c = p6q.tile([P, 1024], U32, name="p6c%d" % u, tag="p6c", align_bytes=64)
                s = p6q.tile([P, 1024], U8, name="p6s%d" % u, tag="p6s", align_bytes=64)
                p6c[u] = (c, s)
            c, s = p6c[u]
            if bb is None:
                nc.vector.quantize_mx(out=c[:].bitcast(FP8X4), scales=s[:], in_=p6[u][:])
                return
            nc.vector.quantize_mx(
                out=c[:, 512 * bb : 512 * bb + 512].bitcast(FP8X4),
                scales=s[:, 512 * bb : 512 * bb + 512],
                in_=p6[u][:, 2048 * bb : 2048 * bb + 2048],
            )

        def tree_a(u, half=None):
            if u < 0 or u >= nu:
                return
            un = units[u]
            if un["kind"] == "leaf":
                par = pt["p5"][:, 512 * un["pj"] : 512 * un["pj"] + 2048].rearrange("p (m q i) -> p m i q", q=2, i=4)
                pg = p6p.tile([P, 4096], BF16, name="p6g%d" % u, tag="p6g", align_bytes=64)
                p6[u] = pg
                nc.vector.tensor_tensor(
                    out=pg[:, 0:2048].rearrange("p (i m q) -> p m i q", i=4, q=2),
                    in0=par,
                    in1=gts[u][:].rearrange("p (m q i) -> p m i q", q=2, i=4),
                    op=ALU.mult,
                )
                if u == nu - 1:
                    quant_p6(u, 0)
                if u in HS:
                    nc.vector.tensor_tensor(
                        out=pg[:, 2048:4096].rearrange("p (i m q) -> p m i q", i=4, q=2),
                        in0=par,
                        in1=hts[u][:].rearrange("p (m q i) -> p m i q", q=2, i=4),
                        op=ALU.mult,
                    )
                    return
                for i0, ni in [(0, 2), (2, 2)] if u == nu - 1 and SPLIT else [(0, 4)]:
                  nc.vector.scalar_tensor_tensor(
                    out=pg[:, 2048:4096].rearrange("p (i m) -> p m i", i=4)[:, :, i0 : i0 + ni],
                    in0=gts[u][:].rearrange("p (m i) -> p m i", i=4)[:, :, i0 : i0 + ni],
                    scalar=1.0,
                    in1=pt["p5"][:, 512 * un["pj"] : 512 * un["pj"] + 2048].rearrange("p (m i) -> p m i", i=4)[:, :, i0 : i0 + ni],
                    op0=ALU.subtract,
                    op1=ALU.mult,
                  )
                return
            if un["cj"] == 0 and not half:
                if un["ch"] == "p4":
                    pt["p4"] = p4p.tile([P, 8192], F32, name="p4")
                else:
                    pt[un["ch"]] = pp.tile([P, 4096], F32, name="%s_%d" % (un["ch"], u), tag="p8")
                    pt5[u] = pt[un["ch"]]
            if un["ch"] == "p5":
                par, lv, rv, gv = p5_views(u, 2)
                nc.vector.tensor_tensor(out=lv, in0=par, in1=gv, op=ALU.mult)
                return
            par, chv, gv = mid_views(u, half)
            nc.vector.tensor_tensor(out=chv[:, :, 0], in0=par, in1=gv, op=ALU.mult)

        def tree_b(u, half=None):
            if u < 0 or u >= nu:
                return
            un = units[u]
            if un["kind"] == "leaf":
                if u != nu - 1:
                    quant_p6(u, None)
                else:
                    for c0, w in [(0, 256), (256, 256)] if SPLIT else [(0, 512)]:
                        c, s = p6c[u]
                        nc.vector.quantize_mx(
                            out=c[:, 512 + c0 : 512 + c0 + w].bitcast(FP8X4),
                            scales=s[:, 512 + c0 : 512 + c0 + w],
                            in_=p6[u][:, 2048 + 4 * c0 : 2048 + 4 * (c0 + w)],
                        )
                return
            if un["ch"] == "p5":
                par, lv, rv, gv = p5_views(u, 1 if u in ET else 2)
                nc.vector.tensor_tensor(out=rv, in0=par, in1=lv, op=ALU.subtract)
                return
            par, chv, gv = mid_views(u, half)
            nc.vector.tensor_tensor(out=chv[:, :, 1], in0=par, in1=chv[:, :, 0], op=ALU.subtract)

        o_t = const.tile([P, 2048], F32, name="o_t")
        last = {}

        def second(u):
            if u < 0 or u >= nu or units[u]["kind"] != "leaf":
                return
            c, s = p6c[u]
            for bb in range(2):
                q = units[u]["q0"] + bb
                if q == 15:
                    for k in range(4):
                        if k == 0 or (k == 2 and SPLIT2):
                            o2 = ps_t.tile([P, 512], F32, name="o2_%d" % k, tag="wt")
                            last[k // 2] = o2
                        cols = slice(512 * bb + 128 * k, 512 * bb + 128 * k + 128)
                        nc.tensor.matmul_mx(
                            out=o2[:, 128 * k : 128 * k + 128],
                            lhsT=c[:, cols].bitcast(FP8X4),
                            lhsT_scale=s[:, cols],
                            rhs=lwc[:, 128 * q : 128 * q + 128].bitcast(FP8X4),
                            rhs_scale=lws[:, 128 * q : 128 * q + 128],
                            start=True,
                            stop=True,
                        )
                    continue
                nc.tensor.matmul_mx(
                    out=o_ps[:],
                    lhsT=lwc[:, 128 * q : 128 * q + 128].bitcast(FP8X4),
                    lhsT_scale=lws[:, 128 * q : 128 * q + 128],
                    rhs=c[:, 512 * bb : 512 * bb + 512].bitcast(FP8X4),
                    rhs_scale=s[:, 512 * bb : 512 * bb + 512],
                    start=(q == 0),
                    stop=(q == 14),
                )
                if q == 14:
                    nc.scalar.copy(out=o_t[:, 0:512], in_=o_ps[:])
                    dummy(WE)
                    o_b = ps_t.tile([P, 512], F32, name="o_b", tag="wt")
                    for k in range(4):
                        nc.tensor.transpose(o_b[:, 128 * k : 128 * k + 128], o_t[:, 128 * k : 128 * k + 128], ident32[:])
                    nc.scalar.copy(out=o_t[:, 512:1024], in_=o_b[:])

        def leaf_tc(piece):
            lg = lgp.tile([P, 2048], BF16, name="lg%d" % piece, tag="lg", align_bytes=64)
            lgs[piece] = lg
            banks = []
            for k in range(2):
                a = 2 * piece + k
                bank = ps_t.tile([P, 1024], BF16, name="lt%d" % a, tag="wt")
                for bb in range(2):
                    for t in range(4):
                        jl = 8 * a + 2 * t + bb - 16 * piece
                        nc.tensor.transpose(bank[:, (4 * bb + t) * 128 : (4 * bb + t) * 128 + 128], lraw[piece][:, 128 * jl : 128 * jl + 128], ident16[:])
                banks.append(bank)
            for k in range(2):
                nc.scalar.copy(
                    out=lg[:, 1024 * k : 1024 * k + 512].rearrange("p (c t) -> p c t", t=4),
                    in_=banks[k][:, 0:512].rearrange("p (t c) -> p c t", t=4),
                )
                nc.scalar.activation(
                    out=lg[:, 1024 * k + 512 : 1024 * k + 1024].rearrange("p (c t) -> p c t", t=4),
                    in_=banks[k][:, 512:1024].rearrange("p (t c) -> p c t", t=4),
                    func=ACT.Copy,
                    scale=-1.0,
                )

        def leaf_q(piece):
            nc.vector.quantize_mx(
                out=lwc[:, 512 * piece : 512 * piece + 512].bitcast(FP8X4),
                scales=lws[:, 512 * piece : 512 * piece + 512],
                in_=lgs[piece][:],
            )

        xraw = rawp.tile([P, 4096], BF16, name="xraw", tag="raw")
        xv = x.rearrange("(k p) d -> p k d", k=4)
        for kk in range(2):
            nc.sync.dma_start(
                out=xraw[:, 2048 * kk : 2048 * kk + 2048].rearrange("p (k d) -> p k d", k=2),
                in_=xv[:, 2 * kk : 2 * kk + 2, :],
            )
        load_w(0)
        load_w(1)
        load_w(2)

        xw = xraw[:].bitcast(F32)
        xg = grpp.tile([P, 2048], F32, name="xg", tag="grp", align_bytes=64)
        for kk in range(2):
            for g in range(2):
                bank = ps_t.tile([P, 512], F32, name="xt%d_%d" % (kk, g), tag="wt")
                for k2 in range(2):
                    for u2 in range(2):
                        src = 512 * (2 * kk + k2) + 256 * g + 128 * u2
                        nc.tensor.transpose(bank[:, (2 * k2 + u2) * 128 : (2 * k2 + u2) * 128 + 128], xw[:, src : src + 128], ident32[:])
                warm_pe(WX)
                dst = xg[:, 1024 * g + 512 * kk : 1024 * g + 512 * kk + 512].rearrange("p (k i u) -> p k i u", k=2, u=2)
                srcv = bank[:].rearrange("p (k u i) -> p k i u", k=2, u=2)
                if g == 0:
                    nc.vector.tensor_copy(out=dst, in_=srcv)
                else:
                    nc.scalar.copy(out=dst, in_=srcv)
        for g in range(2):
            nc.vector.quantize_mx(out=xc[:, 512 * g : 512 * g + 512].bitcast(FP8X4), scales=xs[:, 512 * g : 512 * g + 512], in_=xg[:, 1024 * g : 1024 * g + 1024].bitcast(BF16))

        tr_w(0, 0)
        warm_pe(WW)
        cp_w(0, 0)
        quant_w(0, nodes=(0, 1))
        bt = ps_t.tile([P, 1024], BF16, name="bt", tag="wt")
        nc.tensor.transpose(bt[:, 0:128], brows[:], ident16[:])
        nc.vector.tensor_copy(out=bias[:], in_=bt[:, 0:128])
        tr_w(0, 1)
        warm_pe(WW)
        tr_w(0, 2)
        warm_pe(WW)
        cp_w(0, 1)
        cp_w(0, 2)
        mx_z(0, 0)
        tr_w(1, 0)
        tr_w(1, 1)
        warm_pe(WW)
        quant_w(0, nodes=(1, 2))
        sig(0, 0)
        cp_w(1, 0)
        cp_w(1, 1)
        mx_z(0, 1)
        mx_z(0, 2)
        tr_w(1, 2)
        tr_w(1, 3)
        sig(0, 1)
        sig(0, 2)
        quant_w(1, 0)
        load_w(3)
        cp_w(1, 2)
        cp_w(1, 3)
        mx_z(1, 0)
        mx_z(1, 1)
        tree_a(0)
        quant_w(1, 1)
        tree_b(0)
        load_w(4)
        tr_w(2, 0)
        tr_w(2, 1)
        sig(1, 0)
        sig(1, 1)
        cp_w(2, 0)
        cp_w(2, 1)
        mx_z(1, 2)
        mx_z(1, 3)
        sig(1, 2)
        sig(1, 3)
        tr_w(2, 2)
        tr_w(2, 3)
        cp_w(2, 2)
        cp_w(2, 3)
        load_w(5)
        tree_a(1, 0)
        quant_w(2, 0)
        tree_b(1, 0)
        tr_w(3, 0)
        tr_w(3, 1)
        gates(2, 0)
        quant_w(2, 1)
        tree_a(1, 1)
        tree_b(1, 1)
        cp_w(3, 0)
        cp_w(3, 1)
        tr_w(3, 2)
        tr_w(3, 3)
        gates(2, 1)
        tree_a(2, 0)
        quant_w(3, 0)
        tree_b(2, 0)
        cp_w(3, 2)
        cp_w(3, 3)
        transpose_copy_w(4, 0)
        tree_a(2, 1)
        quant_w(3, 1)
        tree_b(2, 1)
        if not RAMP:
            transpose_copy_w(4, 1)

        for it in range(3, nu + SL):
            if it in LEAF_LOAD_AT:
                load_leaf(LEAF_LOAD_AT.index(it))
            load_w(it + 3)
            for e0 in range(0, 4, RUN):
                es = range(e0, e0 + RUN)
                hx = e0 // RUN
                for j, at in ((0, E0), (1, E1)):
                    if at == hx:
                        tensor_rights(it - EL, j)
                for j, at in ((0, EC0), (1, EC1)):
                    if at == hx:
                        rights_out(it - EL, j)
                if it < nu:
                    for e in es:
                        mx_z(it, e)
                if SECOND_AT in es:
                    second(it - SL)
                if it < nu:
                    for e in es:
                        sig(it, e)
                ahead = [(it + 2, e) for e in es] if it + 2 < nu else []
                if it == 3 and RAMP:
                    ahead = [(4, 2), (4, 3)] if e0 == 0 else [(5, e) for e in range(4)]
                for u, e in ahead:
                    tr_w(u, e)
                for u, e in ahead:
                    cp_w(u, e)
            if it in HS:
                hts[it] = hp.tile([P, 2048], F32, name="h%d" % it, tag="h")
                nc.scalar.activation(out=hts[it][:], in_=gts[it][:], func=ACT.Copy, bias=-1.0, scale=1.0)
            if it in LEAF_WORK_AT:
                leaf_tc(LEAF_WORK_AT.index(it))
            leaf_unit = it - 1 < nu and units[it - 1]["kind"] == "leaf"
            if (leaf_unit or QF) and it != 4:
                quant_w(it + 1)
            halved = it > 3 and it - 1 < nu and units[it - 1]["kind"] == "mid" and (it == 4 or MH == 2) and MH > 0
            if halved:
                for hf in range(2):
                    tree_a(it - 1, hf)
                    if MH == 1:
                        tree_b(it - 1, hf)
            elif it > 3:
                tree_a(it - 1)
            if not (leaf_unit or QF) or it == 4:
                quant_w(it + 1)
            if it - 1 in LEAF_WORK_AT:
                leaf_q(LEAF_WORK_AT.index(it - 1))
            if halved and MH == 2:
                for hf in range(2):
                    tree_b(it - 1, hf)
            elif it > 3 and not halved:
                tree_b(it - 1)

        for c0, w in [(0, 256), (256, 256)] if SPLIT else [(0, 512)]:
            nc.vector.tensor_tensor(
                out=o_t[:, 1536 + c0 : 1536 + c0 + w], in0=o_t[:, 512 + c0 : 512 + c0 + w], in1=(last[0] if c0 == 0 or not SPLIT2 else last[1])[:, c0 : c0 + w], op=ALU.add
            )
        nc.sync.dma_start(
            out=out.rearrange("(p k) c -> p k c", k=4),
            in_=o_t[:, 1536:2048].rearrange("p (k c) -> p k c", k=4),
        )
